import numpy as np
import ml_dtypes


def mxq(x, axis, fmt="e4m3"):
    dtype, down = {"e4m3": (ml_dtypes.float8_e4m3fn, 7), "e5m2": (ml_dtypes.float8_e5m2, 14)}[fmt]
    v = np.moveaxis(np.asarray(x, np.float32).astype(ml_dtypes.bfloat16).astype(np.float64), axis, -1)
    blocks = v.reshape(v.shape[:-1] + (-1, 32))
    amax = np.abs(blocks).max(-1, keepdims=True)
    byte = np.maximum(np.where(amax > 0, np.frexp(amax)[1] - 1 + 127, 0) - down, 1)
    scale = np.exp2(byte - 127.0)
    codes = (blocks / scale).astype(np.float32).astype(dtype).astype(np.float64)
    return np.moveaxis((codes * scale).reshape(v.shape), -1, axis)


WIDE = False


def mx_kscale(k):
    if not WIDE:
        return np.ones(k)
    levels = np.array([10, -10, 5, -5, 0])
    a = np.random.permutation(np.resize(levels, k // 512 * 4)).reshape(k // 512, 4)
    idx = np.arange(k)
    return np.exp2(a[idx // 512, idx % 128 // 32])


BF16 = ml_dtypes.bfloat16


def bf(x):
    return np.asarray(x, np.float32).astype(BF16)


def f64(x):
    return np.asarray(x).astype(np.float64)


E2M1 = np.array([0.0, 0.5, 1.0, 1.5, 2.0, 3.0, 4.0, 6.0, -0.0, -0.5, -1.0, -1.5, -2.0, -3.0, -4.0, -6.0])


def pack_weight(w, fmt):
    k, n = w.shape
    w = f64(bf(w)).reshape(k // 32, 32, n)
    amax = np.abs(w).max(1)
    if fmt == "e4m3":
        byte = np.frexp(amax)[1] - 1 + 127 - 7
    else:
        mant, ex = np.frexp(amax / 6.0)
        byte = np.where(mant > 0.5, ex, ex - 1) + 127
    byte = np.clip(np.where(amax > 0, byte, 1), 1, 254)
    scaled = (w * np.exp2(127.0 - byte)[:, None, :]).reshape(k, n).astype(np.float32)
    by_word = np.ascontiguousarray(scaled.reshape(k // 512, 128, 4, n).transpose(0, 1, 3, 2))
    if fmt == "e4m3":
        words = by_word.astype(ml_dtypes.float8_e4m3fn).view(np.uint8)
    else:
        c = by_word.astype(ml_dtypes.float4_e2m1fn).view(np.uint8) & 0xF
        words = c[..., 0::2] | (c[..., 1::2] << 4)
    return np.ascontiguousarray(words), np.ascontiguousarray(byte.astype(np.uint8).reshape(k // 512, 16, n))


def unpack_weight(words, scales, fmt):
    g, p, n, _ = words.shape
    if fmt == "e4m3":
        vals = np.ascontiguousarray(words).view(ml_dtypes.float8_e4m3fn).astype(np.float64)
    else:
        nib = np.empty((g, p, n, 4), np.uint8)
        nib[..., 0::2] = words & 0xF
        nib[..., 1::2] = words >> 4
        vals = E2M1[nib]
    vals = vals * np.repeat(np.exp2(scales.astype(np.float64) - 127.0), 8, axis=1)[..., None]
    return vals.transpose(0, 1, 3, 2).reshape(g * 512, n)

def pack4(w):
    words, scales = pack_weight(w, "e2m1")
    return words.reshape(words.shape[0], 128, -1), scales


def unpack4(words, scales):
    return unpack_weight(words.reshape(words.shape[0], 128, -1, 2), scales, "e2m1")


B, T, C, H, D, R = 1, 1024, 2048, 16, 128, 512
EPS = 1e-6
THETA = 10000.0


def rmsnorm(v, w):
    var = np.mean(v * v, axis=-1, keepdims=True)
    return v * (1.0 / np.sqrt(var + EPS)) * w


def rope(v, cos, sin):
    re, im = v[..., 0::2], v[..., 1::2]
    c, s = cos[None, :, None, :], sin[None, :, None, :]
    return np.stack([re * c - im * s, re * s + im * c], axis=-1).reshape(v.shape)


def setup_inputs():
    s = mx_kscale(C)
    ang = np.outer(np.arange(T), 1.0 / THETA ** (np.arange(0, D, 2) / D))
    x = bf(np.random.standard_normal((B, T, C)) * s)
    wq = np.random.standard_normal((H * D, C)) / np.sqrt(C) / s[None, :]
    wq_words, wq_scales = pack4(np.ascontiguousarray(wq.T))
    q_norm_w = bf(1.0 + 0.1 * np.random.standard_normal(D))
    return {"x": x,
            "wq_words": wq_words, "wq_scales": wq_scales,
            "q_norm_w": q_norm_w,
            "freqs_cos": bf(np.cos(ang)), "freqs_sin": bf(np.sin(ang))}


def reference(x, wq_words, wq_scales, q_norm_w, freqs_cos, freqs_sin):
    xq = (mxq(f64(x), 2, "e4m3") @ unpack4(wq_words, wq_scales)).reshape(B, T, H, D)
    return rope(rmsnorm(xq, f64(q_norm_w)), f64(freqs_cos), f64(freqs_sin))

@@ -1,0 +1,194 @@
+from contextlib import ExitStack
+
+import concourse.mybir as mybir
+from concourse.masks import make_identity
+
+F32 = mybir.dt.float32
+BF16 = mybir.dt.bfloat16
+I32 = mybir.dt.int32
+U32 = mybir.dt.uint32
+U8 = mybir.dt.uint8
+FP8X4 = mybir.dt.float8_e4m3fn_x4
+FP4X4 = mybir.dt.float4_e2m1fn_x4
+ACT = mybir.ActivationFunctionType
+ALU = mybir.AluOpType
+
+P = 128
+TOKENS = 1024
+K = 2048
+FEATURES = 2048
+HEAD = 128
+PAIRS = HEAD // 2
+EPS = 1e-6
+
+TOKEN_TILES = TOKENS // P
+K_PASS = 4 * P
+PASSES = K // K_PASS
+WORDS = K_PASS // 2
+CHUNK = 512
+CHUNKS = FEATURES // CHUNK
+CHUNK_HEADS = CHUNK // HEAD
+
+FLOPS = 2 * TOKENS * K * FEATURES
+
+
+def tile_mla_pb_kernel(tc, x, wq_words, wq_scales, q_norm_w, freqs_cos, freqs_sin, out):
+    nc = tc.nc
+
+    x_rows = x[0].rearrange("(p i) k -> p i k", i=TOKEN_TILES)
+    out_rows = out[0].rearrange("(p i) h d -> p i (h d)", i=TOKEN_TILES)
+    cos_rows = freqs_cos.rearrange("(p i) j -> p (i j)", i=TOKEN_TILES)
+    sin_rows = freqs_sin.rearrange("(p i) j -> p (i j)", i=TOKEN_TILES)
+    w_words_dram = wq_words.bitcast(I32).rearrange("g p n -> p g n")
+    w_scales_dram = wq_scales.bitcast(I32).rearrange("g q n -> q g n")
+
+    with ExitStack() as ctx:
+        ctx.enter_context(tc.manual_schedule())
+        keep = ctx.enter_context(tc.tile_pool(name="keep", bufs=1))
+        stage = ctx.enter_context(tc.tile_pool(name="stage", bufs=2))
+        small = ctx.enter_context(tc.tile_pool(name="small", bufs=4))
+        work = ctx.enter_context(tc.tile_pool(name="work", bufs=6))
+        xt_pool = ctx.enter_context(tc.psum_pool(name="xt", bufs=2))
+        acc_pool = ctx.enter_context(tc.psum_pool(name="acc", bufs=6))
+
+        x_sb = keep.tile([P, TOKEN_TILES, K], BF16)
+        x_codes = keep.tile([P, TOKEN_TILES, PASSES * P], U32, align_bytes=64)
+        x_scales = keep.tile([P, TOKEN_TILES, PASSES * P], U8, align_bytes=64)
+        w_words = keep.tile([P, CHUNKS, PASSES, 2 * CHUNK], U8, align_bytes=64)
+        w_scales = keep.tile([P, PASSES, FEATURES], U8, align_bytes=64)
+        trig = keep.tile([P, 3, TOKEN_TILES * PAIRS], BF16)
+        table_even = keep.tile([P, TOKEN_TILES, PAIRS, 2], F32)
+        table_odd = keep.tile([P, TOKEN_TILES, PAIRS, 2], F32)
+        gain_even = keep.tile([P, PAIRS, 2], F32)
+        gain_odd = keep.tile([P, PAIRS, 2], F32)
+        gain_row = keep.tile([P, HEAD], BF16)
+        ones = keep.tile([P, P], BF16)
+        ident = keep.tile([P, P], F32)
+        eps = keep.tile([P, 1], F32)
+        warm = keep.tile([P, 1], F32)
+        squares = keep.tile([P, HEAD], F32)
+
+        nc.vector.memset(gain_row[:], 0.0)
+        nc.vector.memset(ones[:], 1.0)
+        nc.vector.memset(eps[:], EPS)
+        nc.vector.memset(w_scales[:].bitcast(I32), 0)
+        make_identity(nc, ident[:])
+
+        nc.scalar.dma_start(out=gain_row[0:1, :], in_=q_norm_w.unsqueeze(0))
+        nc.scalar.dma_start(out=trig[:, 0, :], in_=cos_rows)
+        nc.scalar.dma_start(out=trig[:, 1, :], in_=sin_rows)
+        nc.scalar.dma_start(out=trig[:, 2, :], in_=cos_rows)
+        nc.scalar.activation(out=warm[:], in_=eps[:], func=ACT.Abs_reciprocal_sqrt)
+
+        nc.sync.dma_start(out=x_sb[:, 0, :], in_=x_rows[:, 0, :])
+        nc.sync.dma_start(out=x_sb[:, 1, :], in_=x_rows[:, 1, :])
+        for g in range(0, PASSES, 2):
+            for q in range(8):
+                first = 32 * (q // 4) + q % 4
+                nc.sync.dma_start(
+                    out=w_scales[first:P:64, g : g + 2, :].bitcast(I32),
+                    in_=w_scales_dram[q:16:8, g : g + 2, :],
+                )
+        for c in range(CHUNKS):
+            nc.sync.dma_start(
+                out=w_words[:, c, :, :].bitcast(I32),
+                in_=w_words_dram[:, :, c * CHUNK // 2 : (c + 1) * CHUNK // 2],
+            )
+        for i in range(2, TOKEN_TILES):
+            nc.sync.dma_start(out=x_sb[:, i, :], in_=x_rows[:, i, :])
+
+        gain_ps = acc_pool.tile([P, CHUNK], F32, tag="acc")
+        nc.tensor.matmul(out=gain_ps[:, 0:HEAD], lhsT=ones[:], rhs=gain_row[:], start=True, stop=True)
+        gain_pairs = gain_ps[:, 0:HEAD].rearrange("p (j e) -> p j e", e=2)
+        nc.vector.tensor_copy(out=gain_even[:], in_=gain_pairs[:, :, 0:1].to_broadcast([P, PAIRS, 2]))
+        nc.vector.tensor_scalar_mul(out=gain_odd[:, :, 0:1], in0=gain_pairs[:, :, 1:2], scalar1=-1.0)
+        nc.vector.tensor_copy(out=gain_odd[:, :, 1:2], in_=gain_pairs[:, :, 1:2])
+
+        table_shape = [P, TOKEN_TILES, PAIRS, 2]
+        nc.gpsimd.tensor_tensor(
+            out=table_even[:],
+            in0=trig[:, 0:2, :].rearrange("p e (i j) -> p i j e", i=TOKEN_TILES),
+            in1=gain_even[:].unsqueeze(1).to_broadcast(table_shape),
+            op=ALU.mult,
+        )
+        nc.gpsimd.tensor_tensor(
+            out=table_odd[:],
+            in0=trig[:, 1:3, :].rearrange("p e (i j) -> p i j e", i=TOKEN_TILES),
+            in1=gain_odd[:].unsqueeze(1).to_broadcast(table_shape),
+            op=ALU.mult,
+        )
+
+        def transpose_and_quantise(i):
+            words = x_sb[:, i, :].bitcast(F32)
+            grouped = stage.tile([P, 4 * PASSES * P], BF16, align_bytes=64)
+            grouped_words = grouped[:].bitcast(F32).rearrange("p (g r u) -> p g r u", g=PASSES, u=2)
+            for g0 in range(0, PASSES, 2):
+                xt = xt_pool.tile([P, 2, 2, P], F32)
+                for g in range(g0, g0 + 2):
+                    for u in range(2):
+                        nc.tensor.transpose(
+                            xt[:, g - g0, u, :], words[:, g * WORDS + u : (g + 1) * WORDS : 2], ident[:]
+                        )
+                nc.scalar.copy(
+                    out=grouped_words[:, g0 : g0 + 2, :, :], in_=xt[:].rearrange("p g u r -> p g r u")
+                )
+            nc.vector.quantize_mx(
+                out=x_codes[:, i, :].bitcast(FP8X4), scales=x_scales[:, i, :], in_=grouped[:]
+            )
+
+        def project_and_rotate(i, c):
+            acc = acc_pool.tile([P, CHUNK], F32, tag="acc")
+            for g in range(PASSES):
+                nc.tensor.matmul_mx(
+                    out=acc[:],
+                    lhsT=x_codes[:, i, g * P : (g + 1) * P].bitcast(FP8X4),
+                    lhsT_scale=x_scales[:, i, g * P : (g + 1) * P],
+                    rhs=w_words[:, c, g, :].bitcast(FP4X4),
+                    rhs_scale=w_scales[:, g, c * CHUNK : (c + 1) * CHUNK],
+                    start=(g == 0),
+                    stop=(g == PASSES - 1),
+                )
+            sum_sq = small.tile([P, CHUNK_HEADS], F32)
+            for h in range(CHUNK_HEADS):
+                nc.scalar.activation(
+                    out=squares[:],
+                    in_=acc[:, h * HEAD : (h + 1) * HEAD],
+                    func=ACT.Square,
+                    accum_out=sum_sq[:, h : h + 1],
+                )
+            r = small.tile([P, CHUNK_HEADS], F32)
+            nc.scalar.activation(
+                out=r[:], in_=sum_sq[:], func=ACT.Abs_reciprocal_sqrt, scale=1.0 / HEAD, bias=eps[:]
+            )
+            pairs = acc[:].rearrange("p (h j e) -> p h j e", h=CHUNK_HEADS, e=2)
+            from_even = work.tile([P, CHUNK_HEADS, PAIRS, 2], F32)
+            from_odd = work.tile([P, CHUNK_HEADS, PAIRS, 2], F32)
+            for h in range(CHUNK_HEADS):
+                nc.vector.scalar_tensor_tensor(
+                    out=from_even[:, h, :, :],
+                    in0=pairs[:, h, :, 0:1].to_broadcast([P, PAIRS, 2]),
+                    scalar=r[:, h : h + 1],
+                    in1=table_even[:, i, :, :],
+                    op0=ALU.mult,
+                    op1=ALU.mult,
+                )
+                nc.vector.scalar_tensor_tensor(
+                    out=from_odd[:, h, :, :],
+                    in0=pairs[:, h, :, 1:2].to_broadcast([P, PAIRS, 2]),
+                    scalar=r[:, h : h + 1],
+                    in1=table_odd[:, i, :, :],
+                    op0=ALU.mult,
+                    op1=ALU.mult,
+                )
+            nc.gpsimd.tensor_tensor(out=from_even[:], in0=from_even[:], in1=from_odd[:], op=ALU.add)
+            nc.sync.dma_start(
+                out=out_rows[:, i, c * CHUNK : (c + 1) * CHUNK],
+                in_=from_even[:].rearrange("p h j e -> p (h j e)"),
+            )
+
+        transpose_and_quantise(0)
+        for i in range(TOKEN_TILES):
+            if i + 1 < TOKEN_TILES:
+                transpose_and_quantise(i + 1)
+            for c in range(CHUNKS):
+                project_and_rotate(i, c)

@@ -180,7 +180,7 @@ def tile_mla_pb_kernel(tc, x, wq_words, wq_scales, q_norm_w, freqs_cos, freqs_si
                     op0=ALU.mult,
                     op1=ALU.mult,
                 )
-            nc.gpsimd.tensor_tensor(out=from_even[:], in0=from_even[:], in1=from_odd[:], op=ALU.add)
+            nc.vector.tensor_tensor(out=from_even[:], in0=from_even[:], in1=from_odd[:], op=ALU.add)
             nc.sync.dma_start(
                 out=out_rows[:, i, c * CHUNK : (c + 1) * CHUNK],
                 in_=from_even[:].rearrange("p h j e -> p (h j e)"),

@@ -46,8 +46,8 @@ def tile_mla_pb_kernel(tc, x, wq_words, wq_scales, q_norm_w, freqs_cos, freqs_si
         ctx.enter_context(tc.manual_schedule())
         keep = ctx.enter_context(tc.tile_pool(name="keep", bufs=1))
         stage = ctx.enter_context(tc.tile_pool(name="stage", bufs=2))
-        small = ctx.enter_context(tc.tile_pool(name="small", bufs=4))
-        work = ctx.enter_context(tc.tile_pool(name="work", bufs=6))
+        small = ctx.enter_context(tc.tile_pool(name="small", bufs=8))
+        work = ctx.enter_context(tc.tile_pool(name="work", bufs=12))
         xt_pool = ctx.enter_context(tc.psum_pool(name="xt", bufs=2))
         acc_pool = ctx.enter_context(tc.psum_pool(name="acc", bufs=6))
 
@@ -104,19 +104,20 @@ def tile_mla_pb_kernel(tc, x, wq_words, wq_scales, q_norm_w, freqs_cos, freqs_si
         nc.vector.tensor_scalar_mul(out=gain_odd[:, :, 0:1], in0=gain_pairs[:, :, 1:2], scalar1=-1.0)
         nc.vector.tensor_copy(out=gain_odd[:, :, 1:2], in_=gain_pairs[:, :, 1:2])
 
-        table_shape = [P, TOKEN_TILES, PAIRS, 2]
-        nc.gpsimd.tensor_tensor(
-            out=table_even[:],
-            in0=trig[:, 0:2, :].rearrange("p e (i j) -> p i j e", i=TOKEN_TILES),
-            in1=gain_even[:].unsqueeze(1).to_broadcast(table_shape),
-            op=ALU.mult,
-        )
-        nc.gpsimd.tensor_tensor(
-            out=table_odd[:],
-            in0=trig[:, 1:3, :].rearrange("p e (i j) -> p i j e", i=TOKEN_TILES),
-            in1=gain_odd[:].unsqueeze(1).to_broadcast(table_shape),
-            op=ALU.mult,
-        )
+        def build_tables():
+            table_shape = [P, TOKEN_TILES, PAIRS, 2]
+            nc.vector.tensor_tensor(
+                out=table_even[:],
+                in0=trig[:, 0:2, :].rearrange("p e (i j) -> p i j e", i=TOKEN_TILES),
+                in1=gain_even[:].unsqueeze(1).to_broadcast(table_shape),
+                op=ALU.mult,
+            )
+            nc.vector.tensor_tensor(
+                out=table_odd[:],
+                in0=trig[:, 1:3, :].rearrange("p e (i j) -> p i j e", i=TOKEN_TILES),
+                in1=gain_odd[:].unsqueeze(1).to_broadcast(table_shape),
+                op=ALU.mult,
+            )
 
         def transpose_and_quantise(i):
             words = x_sb[:, i, :].bitcast(F32)
@@ -180,13 +181,14 @@ def tile_mla_pb_kernel(tc, x, wq_words, wq_scales, q_norm_w, freqs_cos, freqs_si
                     op0=ALU.mult,
                     op1=ALU.mult,
                 )
-            nc.vector.tensor_tensor(out=from_even[:], in0=from_even[:], in1=from_odd[:], op=ALU.add)
+            nc.gpsimd.tensor_tensor(out=from_even[:], in0=from_even[:], in1=from_odd[:], op=ALU.add)
             nc.sync.dma_start(
                 out=out_rows[:, i, c * CHUNK : (c + 1) * CHUNK],
                 in_=from_even[:].rearrange("p h j e -> p (h j e)"),
             )
 
         transpose_and_quantise(0)
+        build_tables()
         for i in range(TOKEN_TILES):
             if i + 1 < TOKEN_TILES:
                 transpose_and_quantise(i + 1)

@@ -181,7 +181,8 @@ def tile_mla_pb_kernel(tc, x, wq_words, wq_scales, q_norm_w, freqs_cos, freqs_si
                     op0=ALU.mult,
                     op1=ALU.mult,
                 )
-            nc.gpsimd.tensor_tensor(out=from_even[:], in0=from_even[:], in1=from_odd[:], op=ALU.add)
+            adder = nc.gpsimd if c % 2 == 0 else nc.vector
+            adder.tensor_tensor(out=from_even[:], in0=from_even[:], in1=from_odd[:], op=ALU.add)
             nc.sync.dma_start(
                 out=out_rows[:, i, c * CHUNK : (c + 1) * CHUNK],
                 in_=from_even[:].rearrange("p h j e -> p (h j e)"),

@@ -130,7 +130,7 @@ def tile_mla_pb_kernel(tc, x, wq_words, wq_scales, q_norm_w, freqs_cos, freqs_si
                         nc.tensor.transpose(
                             xt[:, g - g0, u, :], words[:, g * WORDS + u : (g + 1) * WORDS : 2], ident[:]
                         )
-                nc.scalar.copy(
+                nc.vector.tensor_copy(
                     out=grouped_words[:, g0 : g0 + 2, :, :], in_=xt[:].rearrange("p g u r -> p g r u")
                 )
             nc.vector.quantize_mx(
@@ -181,8 +181,7 @@ def tile_mla_pb_kernel(tc, x, wq_words, wq_scales, q_norm_w, freqs_cos, freqs_si
                     op0=ALU.mult,
                     op1=ALU.mult,
                 )
-            adder = nc.gpsimd if c % 2 == 0 else nc.vector
-            adder.tensor_tensor(out=from_even[:], in0=from_even[:], in1=from_odd[:], op=ALU.add)
+            nc.gpsimd.tensor_tensor(out=from_even[:], in0=from_even[:], in1=from_odd[:], op=ALU.add)
             nc.sync.dma_start(
                 out=out_rows[:, i, c * CHUNK : (c + 1) * CHUNK],
                 in_=from_even[:].rearrange("p h j e -> p (h j e)"),

@@ -28,6 +28,7 @@ WORDS = K_PASS // 2
 CHUNK = 512
 CHUNKS = FEATURES // CHUNK
 CHUNK_HEADS = CHUNK // HEAD
+PREPARE_AFTER = 1
 
 FLOPS = 2 * TOKENS * K * FEATURES
 
@@ -47,7 +48,7 @@ def tile_mla_pb_kernel(tc, x, wq_words, wq_scales, q_norm_w, freqs_cos, freqs_si
         keep = ctx.enter_context(tc.tile_pool(name="keep", bufs=1))
         stage = ctx.enter_context(tc.tile_pool(name="stage", bufs=2))
         small = ctx.enter_context(tc.tile_pool(name="small", bufs=8))
-        work = ctx.enter_context(tc.tile_pool(name="work", bufs=12))
+        work = ctx.enter_context(tc.tile_pool(name="work", bufs=8))
         xt_pool = ctx.enter_context(tc.psum_pool(name="xt", bufs=2))
         acc_pool = ctx.enter_context(tc.psum_pool(name="acc", bufs=6))
 
@@ -56,11 +57,9 @@ def tile_mla_pb_kernel(tc, x, wq_words, wq_scales, q_norm_w, freqs_cos, freqs_si
         x_scales = keep.tile([P, TOKEN_TILES, PASSES * P], U8, align_bytes=64)
         w_words = keep.tile([P, CHUNKS, PASSES, 2 * CHUNK], U8, align_bytes=64)
         w_scales = keep.tile([P, PASSES, FEATURES], U8, align_bytes=64)
-        trig = keep.tile([P, 3, TOKEN_TILES * PAIRS], BF16)
-        table_even = keep.tile([P, TOKEN_TILES, PAIRS, 2], F32)
-        table_odd = keep.tile([P, TOKEN_TILES, PAIRS, 2], F32)
-        gain_even = keep.tile([P, PAIRS, 2], F32)
-        gain_odd = keep.tile([P, PAIRS, 2], F32)
+        trig = keep.tile([P, 4, TOKEN_TILES * PAIRS], BF16)
+        factors = keep.tile([P, PAIRS, 2, 2], F32)
+        table = keep.tile([P, TOKEN_TILES, PAIRS, 2, 2], F32)
         gain_row = keep.tile([P, HEAD], BF16)
         ones = keep.tile([P, P], BF16)
         ident = keep.tile([P, P], F32)
@@ -71,51 +70,54 @@ def tile_mla_pb_kernel(tc, x, wq_words, wq_scales, q_norm_w, freqs_cos, freqs_si
         nc.vector.memset(gain_row[:], 0.0)
         nc.vector.memset(ones[:], 1.0)
         nc.vector.memset(eps[:], EPS)
-        nc.vector.memset(w_scales[:].bitcast(I32), 0)
+        for c in range(CHUNKS):
+            nc.vector.memset(w_scales[:, :, c * CHUNK : (c + 1) * CHUNK].bitcast(I32), 0)
         make_identity(nc, ident[:])
 
-        nc.scalar.dma_start(out=gain_row[0:1, :], in_=q_norm_w.unsqueeze(0))
-        nc.scalar.dma_start(out=trig[:, 0, :], in_=cos_rows)
-        nc.scalar.dma_start(out=trig[:, 1, :], in_=sin_rows)
-        nc.scalar.dma_start(out=trig[:, 2, :], in_=cos_rows)
-        nc.scalar.activation(out=warm[:], in_=eps[:], func=ACT.Abs_reciprocal_sqrt)
+        def load_x(i):
+            nc.sync.dma_start(out=x_sb[:, i, :], in_=x_rows[:, i, :])
 
-        nc.sync.dma_start(out=x_sb[:, 0, :], in_=x_rows[:, 0, :])
-        nc.sync.dma_start(out=x_sb[:, 1, :], in_=x_rows[:, 1, :])
-        for g in range(0, PASSES, 2):
-            for q in range(8):
-                first = 32 * (q // 4) + q % 4
+        def load_w(c):
+            for r in range(4):
                 nc.sync.dma_start(
-                    out=w_scales[first:P:64, g : g + 2, :].bitcast(I32),
-                    in_=w_scales_dram[q:16:8, g : g + 2, :],
+                    out=w_scales[r:P:32, :, c * CHUNK : (c + 1) * CHUNK].bitcast(I32),
+                    in_=w_scales_dram[r:16:4, :, c * CHUNK // 4 : (c + 1) * CHUNK // 4],
                 )
-        for c in range(CHUNKS):
             nc.sync.dma_start(
                 out=w_words[:, c, :, :].bitcast(I32),
                 in_=w_words_dram[:, :, c * CHUNK // 2 : (c + 1) * CHUNK // 2],
             )
+
+        nc.scalar.dma_start(out=gain_row[0:1, :], in_=q_norm_w.unsqueeze(0))
+        nc.scalar.activation(out=warm[:], in_=eps[:], func=ACT.Abs_reciprocal_sqrt)
+        load_x(0)
+        load_w(0)
+        nc.sync.dma_start(out=trig[:, 0, :], in_=cos_rows)
+        nc.sync.dma_start(out=trig[:, 1, :], in_=sin_rows)
+        nc.sync.dma_start(out=trig[:, 2, :], in_=sin_rows)
+        nc.sync.dma_start(out=trig[:, 3, :], in_=cos_rows)
+        load_w(1)
+        load_x(1)
+        load_w(2)
+        load_w(3)
         for i in range(2, TOKEN_TILES):
-            nc.sync.dma_start(out=x_sb[:, i, :], in_=x_rows[:, i, :])
+            load_x(i)
 
         gain_ps = acc_pool.tile([P, CHUNK], F32, tag="acc")
         nc.tensor.matmul(out=gain_ps[:, 0:HEAD], lhsT=ones[:], rhs=gain_row[:], start=True, stop=True)
-        gain_pairs = gain_ps[:, 0:HEAD].rearrange("p (j e) -> p j e", e=2)
-        nc.vector.tensor_copy(out=gain_even[:], in_=gain_pairs[:, :, 0:1].to_broadcast([P, PAIRS, 2]))
-        nc.vector.tensor_scalar_mul(out=gain_odd[:, :, 0:1], in0=gain_pairs[:, :, 1:2], scalar1=-1.0)
-        nc.vector.tensor_copy(out=gain_odd[:, :, 1:2], in_=gain_pairs[:, :, 1:2])
+        gain_pairs = gain_ps[:, 0:HEAD].rearrange("p (j s) -> p j s", s=2)
+        nc.vector.tensor_copy(out=factors[:, :, :, 1], in_=gain_pairs)
+        nc.vector.tensor_copy(out=factors[:, :, 0, 0], in_=gain_pairs[:, :, 0])
+        nc.vector.tensor_scalar_mul(out=factors[:, :, 1, 0], in0=gain_pairs[:, :, 1], scalar1=-1.0)
 
-        def build_tables():
-            table_shape = [P, TOKEN_TILES, PAIRS, 2]
+        def build_table():
             nc.vector.tensor_tensor(
-                out=table_even[:],
-                in0=trig[:, 0:2, :].rearrange("p e (i j) -> p i j e", i=TOKEN_TILES),
-                in1=gain_even[:].unsqueeze(1).to_broadcast(table_shape),
-                op=ALU.mult,
-            )
-            nc.vector.tensor_tensor(
-                out=table_odd[:],
-                in0=trig[:, 1:3, :].rearrange("p e (i j) -> p i j e", i=TOKEN_TILES),
-                in1=gain_odd[:].unsqueeze(1).to_broadcast(table_shape),
+                out=table[:].rearrange("p i j s e -> p i j (s e)"),
+                in0=trig[:].rearrange("p f (i j) -> p i j f", i=TOKEN_TILES),
+                in1=factors[:]
+                .rearrange("p j s e -> p j (s e)")
+                .unsqueeze(1)
+                .to_broadcast([P, TOKEN_TILES, PAIRS, 4]),
                 op=ALU.mult,
             )
 
@@ -137,7 +139,7 @@ def tile_mla_pb_kernel(tc, x, wq_words, wq_scales, q_norm_w, freqs_cos, freqs_si
                 out=x_codes[:, i, :].bitcast(FP8X4), scales=x_scales[:, i, :], in_=grouped[:]
             )
 
-        def project_and_rotate(i, c):
+        def project(i, c):
             acc = acc_pool.tile([P, CHUNK], F32, tag="acc")
             for g in range(PASSES):
                 nc.tensor.matmul_mx(
@@ -157,40 +159,41 @@ def tile_mla_pb_kernel(tc, x, wq_words, wq_scales, q_norm_w, freqs_cos, freqs_si
                     func=ACT.Square,
                     accum_out=sum_sq[:, h : h + 1],
                 )
+            return i, c, acc, sum_sq
+
+        def rotate(i, c, acc, sum_sq):
             r = small.tile([P, CHUNK_HEADS], F32)
             nc.scalar.activation(
                 out=r[:], in_=sum_sq[:], func=ACT.Abs_reciprocal_sqrt, scale=1.0 / HEAD, bias=eps[:]
             )
-            pairs = acc[:].rearrange("p (h j e) -> p h j e", h=CHUNK_HEADS, e=2)
-            from_even = work.tile([P, CHUNK_HEADS, PAIRS, 2], F32)
-            from_odd = work.tile([P, CHUNK_HEADS, PAIRS, 2], F32)
+            products = work.tile([P, CHUNK_HEADS, PAIRS, 2, 2], F32)
             for h in range(CHUNK_HEADS):
                 nc.vector.scalar_tensor_tensor(
-                    out=from_even[:, h, :, :],
-                    in0=pairs[:, h, :, 0:1].to_broadcast([P, PAIRS, 2]),
+                    out=products[:, h].rearrange("p j s e -> p (j s) e"),
+                    in0=acc[:, h * HEAD : (h + 1) * HEAD].unsqueeze(2).to_broadcast([P, HEAD, 2]),
                     scalar=r[:, h : h + 1],
-                    in1=table_even[:, i, :, :],
+                    in1=table[:, i].rearrange("p j s e -> p (j s) e"),
                     op0=ALU.mult,
                     op1=ALU.mult,
                 )
-                nc.vector.scalar_tensor_tensor(
-                    out=from_odd[:, h, :, :],
-                    in0=pairs[:, h, :, 1:2].to_broadcast([P, PAIRS, 2]),
-                    scalar=r[:, h : h + 1],
-                    in1=table_odd[:, i, :, :],
-                    op0=ALU.mult,
-                    op1=ALU.mult,
-                )
-            nc.gpsimd.tensor_tensor(out=from_even[:], in0=from_even[:], in1=from_odd[:], op=ALU.add)
+            rotated = work.tile([P, CHUNK_HEADS, PAIRS, 2], F32)
+            nc.gpsimd.tensor_tensor(
+                out=rotated[:], in0=products[:, :, :, 0, :], in1=products[:, :, :, 1, :], op=ALU.add
+            )
             nc.sync.dma_start(
                 out=out_rows[:, i, c * CHUNK : (c + 1) * CHUNK],
-                in_=from_even[:].rearrange("p h j e -> p (h j e)"),
+                in_=rotated[:].rearrange("p h j e -> p (h j e)"),
             )
 
         transpose_and_quantise(0)
-        build_tables()
+        build_table()
+        waiting = None
         for i in range(TOKEN_TILES):
-            if i + 1 < TOKEN_TILES:
-                transpose_and_quantise(i + 1)
             for c in range(CHUNKS):
-                project_and_rotate(i, c)
+                projected = project(i, c)
+                if waiting is not None:
+                    rotate(*waiting)
+                waiting = projected
+                if c == PREPARE_AFTER and i + 1 < TOKEN_TILES:
+                    transpose_and_quantise(i + 1)
+        rotate(*waiting)

@@ -28,7 +28,6 @@ WORDS = K_PASS // 2
 CHUNK = 512
 CHUNKS = FEATURES // CHUNK
 CHUNK_HEADS = CHUNK // HEAD
-PREPARE_AFTER = 1
 
 FLOPS = 2 * TOKENS * K * FEATURES
 
@@ -70,36 +69,38 @@ def tile_mla_pb_kernel(tc, x, wq_words, wq_scales, q_norm_w, freqs_cos, freqs_si
         nc.vector.memset(gain_row[:], 0.0)
         nc.vector.memset(ones[:], 1.0)
         nc.vector.memset(eps[:], EPS)
-        for c in range(CHUNKS):
-            nc.vector.memset(w_scales[:, :, c * CHUNK : (c + 1) * CHUNK].bitcast(I32), 0)
+        nc.vector.memset(w_scales[:].bitcast(I32), 0)
         make_identity(nc, ident[:])
 
         def load_x(i):
             nc.sync.dma_start(out=x_sb[:, i, :], in_=x_rows[:, i, :])
 
+        def load_w_scales():
+            for g in range(0, PASSES, 2):
+                for q in range(8):
+                    first = 32 * (q // 4) + q % 4
+                    nc.sync.dma_start(
+                        out=w_scales[first:P:64, g : g + 2, :].bitcast(I32),
+                        in_=w_scales_dram[q:16:8, g : g + 2, :],
+                    )
+
         def load_w(c):
-            for r in range(4):
-                nc.sync.dma_start(
-                    out=w_scales[r:P:32, :, c * CHUNK : (c + 1) * CHUNK].bitcast(I32),
-                    in_=w_scales_dram[r:16:4, :, c * CHUNK // 4 : (c + 1) * CHUNK // 4],
-                )
             nc.sync.dma_start(
                 out=w_words[:, c, :, :].bitcast(I32),
                 in_=w_words_dram[:, :, c * CHUNK // 2 : (c + 1) * CHUNK // 2],
             )
 
         nc.scalar.dma_start(out=gain_row[0:1, :], in_=q_norm_w.unsqueeze(0))
+        nc.scalar.dma_start(out=trig[:, 0, :], in_=cos_rows)
+        nc.scalar.dma_start(out=trig[:, 1, :], in_=sin_rows)
+        nc.scalar.dma_start(out=trig[:, 2, :], in_=sin_rows)
+        nc.scalar.dma_start(out=trig[:, 3, :], in_=cos_rows)
         nc.scalar.activation(out=warm[:], in_=eps[:], func=ACT.Abs_reciprocal_sqrt)
         load_x(0)
-        load_w(0)
-        nc.sync.dma_start(out=trig[:, 0, :], in_=cos_rows)
-        nc.sync.dma_start(out=trig[:, 1, :], in_=sin_rows)
-        nc.sync.dma_start(out=trig[:, 2, :], in_=sin_rows)
-        nc.sync.dma_start(out=trig[:, 3, :], in_=cos_rows)
-        load_w(1)
         load_x(1)
-        load_w(2)
-        load_w(3)
+        load_w_scales()
+        for c in range(CHUNKS):
+            load_w(c)
         for i in range(2, TOKEN_TILES):
             load_x(i)
 
@@ -189,11 +190,11 @@ def tile_mla_pb_kernel(tc, x, wq_words, wq_scales, q_norm_w, freqs_cos, freqs_si
         build_table()
         waiting = None
         for i in range(TOKEN_TILES):
+            if i + 1 < TOKEN_TILES:
+                transpose_and_quantise(i + 1)
             for c in range(CHUNKS):
                 projected = project(i, c)
                 if waiting is not None:
                     rotate(*waiting)
                 waiting = projected
-                if c == PREPARE_AFTER and i + 1 < TOKEN_TILES:
-                    transpose_and_quantise(i + 1)
         rotate(*waiting)

@@ -133,9 +133,14 @@ def tile_mla_pb_kernel(tc, x, wq_words, wq_scales, q_norm_w, freqs_cos, freqs_si
                         nc.tensor.transpose(
                             xt[:, g - g0, u, :], words[:, g * WORDS + u : (g + 1) * WORDS : 2], ident[:]
                         )
-                nc.vector.tensor_copy(
-                    out=grouped_words[:, g0 : g0 + 2, :, :], in_=xt[:].rearrange("p g u r -> p g r u")
-                )
+                if g0 == 0:
+                    nc.vector.tensor_copy(
+                        out=grouped_words[:, g0 : g0 + 2, :, :], in_=xt[:].rearrange("p g u r -> p g r u")
+                    )
+                else:
+                    nc.scalar.copy(
+                        out=grouped_words[:, g0 : g0 + 2, :, :], in_=xt[:].rearrange("p g u r -> p g r u")
+                    )
             nc.vector.quantize_mx(
                 out=x_codes[:, i, :].bitcast(FP8X4), scales=x_scales[:, i, :], in_=grouped[:]
             )

@@ -28,6 +28,7 @@ WORDS = K_PASS // 2
 CHUNK = 512
 CHUNKS = FEATURES // CHUNK
 CHUNK_HEADS = CHUNK // HEAD
+SQUARE_SLOTS = 8
 
 FLOPS = 2 * TOKENS * K * FEATURES
 
@@ -64,7 +65,7 @@ def tile_mla_pb_kernel(tc, x, wq_words, wq_scales, q_norm_w, freqs_cos, freqs_si
         ident = keep.tile([P, P], F32)
         eps = keep.tile([P, 1], F32)
         warm = keep.tile([P, 1], F32)
-        squares = keep.tile([P, HEAD], F32)
+        squares = keep.tile([P, SQUARE_SLOTS, HEAD], F32)
 
         nc.vector.memset(gain_row[:], 0.0)
         nc.vector.memset(ones[:], 1.0)
@@ -160,7 +161,7 @@ def tile_mla_pb_kernel(tc, x, wq_words, wq_scales, q_norm_w, freqs_cos, freqs_si
             sum_sq = small.tile([P, CHUNK_HEADS], F32)
             for h in range(CHUNK_HEADS):
                 nc.scalar.activation(
-                    out=squares[:],
+                    out=squares[:, (c * CHUNK_HEADS + h) % SQUARE_SLOTS, :],
                     in_=acc[:, h * HEAD : (h + 1) * HEAD],
                     func=ACT.Square,
                     accum_out=sum_sq[:, h : h + 1],

@@ -134,14 +134,9 @@ def tile_mla_pb_kernel(tc, x, wq_words, wq_scales, q_norm_w, freqs_cos, freqs_si
                         nc.tensor.transpose(
                             xt[:, g - g0, u, :], words[:, g * WORDS + u : (g + 1) * WORDS : 2], ident[:]
                         )
-                if g0 == 0:
-                    nc.vector.tensor_copy(
-                        out=grouped_words[:, g0 : g0 + 2, :, :], in_=xt[:].rearrange("p g u r -> p g r u")
-                    )
-                else:
-                    nc.scalar.copy(
-                        out=grouped_words[:, g0 : g0 + 2, :, :], in_=xt[:].rearrange("p g u r -> p g r u")
-                    )
+                nc.scalar.copy(
+                    out=grouped_words[:, g0 : g0 + 2, :, :], in_=xt[:].rearrange("p g u r -> p g r u")
+                )
             nc.vector.quantize_mx(
                 out=x_codes[:, i, :].bitcast(FP8X4), scales=x_scales[:, i, :], in_=grouped[:]
             )

@@ -67,23 +67,18 @@ def tile_mla_pb_kernel(tc, x, wq_words, wq_scales, q_norm_w, freqs_cos, freqs_si
         warm = keep.tile([P, 1], F32)
         squares = keep.tile([P, SQUARE_SLOTS, HEAD], F32)
 
-        nc.vector.memset(gain_row[:], 0.0)
-        nc.vector.memset(ones[:], 1.0)
         nc.vector.memset(eps[:], EPS)
+        nc.vector.memset(gain_row[:], 0.0)
         nc.vector.memset(w_scales[:].bitcast(I32), 0)
+        nc.vector.memset(ones[:], 1.0)
         make_identity(nc, ident[:])
 
         def load_x(i):
             nc.sync.dma_start(out=x_sb[:, i, :], in_=x_rows[:, i, :])
 
         def load_w_scales():
-            for g in range(0, PASSES, 2):
-                for q in range(8):
-                    first = 32 * (q // 4) + q % 4
-                    nc.sync.dma_start(
-                        out=w_scales[first:P:64, g : g + 2, :].bitcast(I32),
-                        in_=w_scales_dram[q:16:8, g : g + 2, :],
-                    )
+            for r in range(4):
+                nc.sync.dma_start(out=w_scales[r:P:32, :, :].bitcast(I32), in_=w_scales_dram[r:16:4, :, :])
 
         def load_w(c):
             nc.sync.dma_start(
@@ -91,28 +86,31 @@ def tile_mla_pb_kernel(tc, x, wq_words, wq_scales, q_norm_w, freqs_cos, freqs_si
                 in_=w_words_dram[:, :, c * CHUNK // 2 : (c + 1) * CHUNK // 2],
             )
 
+        load_x(0)
+        load_w(0)
+        load_w_scales()
         nc.scalar.dma_start(out=gain_row[0:1, :], in_=q_norm_w.unsqueeze(0))
         nc.scalar.dma_start(out=trig[:, 0, :], in_=cos_rows)
-        nc.scalar.dma_start(out=trig[:, 1, :], in_=sin_rows)
-        nc.scalar.dma_start(out=trig[:, 2, :], in_=sin_rows)
-        nc.scalar.dma_start(out=trig[:, 3, :], in_=cos_rows)
         nc.scalar.activation(out=warm[:], in_=eps[:], func=ACT.Abs_reciprocal_sqrt)
-        load_x(0)
+        nc.scalar.dma_start(out=trig[:, 1, :], in_=sin_rows)
+        load_w(1)
         load_x(1)
-        load_w_scales()
-        for c in range(CHUNKS):
-            load_w(c)
+        load_w(2)
+        load_w(3)
         for i in range(2, TOKEN_TILES):
             load_x(i)
 
-        gain_ps = acc_pool.tile([P, CHUNK], F32, tag="acc")
-        nc.tensor.matmul(out=gain_ps[:, 0:HEAD], lhsT=ones[:], rhs=gain_row[:], start=True, stop=True)
-        gain_pairs = gain_ps[:, 0:HEAD].rearrange("p (j s) -> p j s", s=2)
-        nc.vector.tensor_copy(out=factors[:, :, :, 1], in_=gain_pairs)
-        nc.vector.tensor_copy(out=factors[:, :, 0, 0], in_=gain_pairs[:, :, 0])
-        nc.vector.tensor_scalar_mul(out=factors[:, :, 1, 0], in0=gain_pairs[:, :, 1], scalar1=-1.0)
+        def spread_gain():
+            gain_ps = acc_pool.tile([P, CHUNK], F32, tag="acc")
+            nc.tensor.matmul(out=gain_ps[:, 0:HEAD], lhsT=ones[:], rhs=gain_row[:], start=True, stop=True)
+            gain_pairs = gain_ps[:, 0:HEAD].rearrange("p (j s) -> p j s", s=2)
+            nc.vector.tensor_copy(out=factors[:, :, :, 1], in_=gain_pairs)
+            nc.vector.tensor_copy(out=factors[:, :, 0, 0], in_=gain_pairs[:, :, 0])
+            nc.vector.tensor_scalar_mul(out=factors[:, :, 1, 0], in0=gain_pairs[:, :, 1], scalar1=-1.0)
 
         def build_table():
+            nc.scalar.copy(out=trig[:, 2, :], in_=trig[:, 1, :])
+            nc.scalar.copy(out=trig[:, 3, :], in_=trig[:, 0, :])
             nc.vector.tensor_tensor(
                 out=table[:].rearrange("p i j s e -> p i j (s e)"),
                 in0=trig[:].rearrange("p f (i j) -> p i j f", i=TOKEN_TILES),
@@ -188,14 +186,18 @@ def tile_mla_pb_kernel(tc, x, wq_words, wq_scales, q_norm_w, freqs_cos, freqs_si
             )
 
         transpose_and_quantise(0)
+        spread_gain()
         build_table()
         waiting = None
         for i in range(TOKEN_TILES):
-            if i + 1 < TOKEN_TILES:
-                transpose_and_quantise(i + 1)
             for c in range(CHUNKS):
                 projected = project(i, c)
                 if waiting is not None:
                     rotate(*waiting)
                 waiting = projected
+                if i == 0 and c == 0:
+                    rotate(*waiting)
+                    waiting = None
+                if c == 1 and i + 1 < TOKEN_TILES:
+                    transpose_and_quantise(i + 1)
         rotate(*waiting)

@@ -198,6 +198,8 @@ def tile_mla_pb_kernel(tc, x, wq_words, wq_scales, q_norm_w, freqs_cos, freqs_si
                 if i == 0 and c == 0:
                     rotate(*waiting)
                     waiting = None
-                if c == 1 and i + 1 < TOKEN_TILES:
-                    transpose_and_quantise(i + 1)
+                if i == 0 and c == 1:
+                    transpose_and_quantise(1)
+                if c == CHUNKS - 1 and i + 2 < TOKEN_TILES:
+                    transpose_and_quantise(i + 2)
         rotate(*waiting)

@@ -37,7 +37,7 @@ def tile_mla_pb_kernel(tc, x, wq_words, wq_scales, q_norm_w, freqs_cos, freqs_si
     nc = tc.nc
 
     x_rows = x[0].rearrange("(p i) k -> p i k", i=TOKEN_TILES)
-    out_rows = out[0].rearrange("(p i) h d -> p i (h d)", i=TOKEN_TILES)
+    out_flat = out[0].rearrange("(p i) h d -> p (i h d)", i=TOKEN_TILES)
     cos_rows = freqs_cos.rearrange("(p i) j -> p (i j)", i=TOKEN_TILES)
     sin_rows = freqs_sin.rearrange("(p i) j -> p (i j)", i=TOKEN_TILES)
     w_words_dram = wq_words.bitcast(I32).rearrange("g p n -> p g n")
@@ -48,7 +48,7 @@ def tile_mla_pb_kernel(tc, x, wq_words, wq_scales, q_norm_w, freqs_cos, freqs_si
         keep = ctx.enter_context(tc.tile_pool(name="keep", bufs=1))
         stage = ctx.enter_context(tc.tile_pool(name="stage", bufs=2))
         small = ctx.enter_context(tc.tile_pool(name="small", bufs=8))
-        work = ctx.enter_context(tc.tile_pool(name="work", bufs=8))
+        work = ctx.enter_context(tc.tile_pool(name="work", bufs=4))
         xt_pool = ctx.enter_context(tc.psum_pool(name="xt", bufs=2))
         acc_pool = ctx.enter_context(tc.psum_pool(name="acc", bufs=6))
 
@@ -161,28 +161,41 @@ def tile_mla_pb_kernel(tc, x, wq_words, wq_scales, q_norm_w, freqs_cos, freqs_si
                 )
             return i, c, acc, sum_sq
 
+        filling = {}
+
         def rotate(i, c, acc, sum_sq):
+            number = i * CHUNKS + c
+            place = (number + 1) % 2
             r = small.tile([P, CHUNK_HEADS], F32)
             nc.scalar.activation(
                 out=r[:], in_=sum_sq[:], func=ACT.Abs_reciprocal_sqrt, scale=1.0 / HEAD, bias=eps[:]
             )
-            products = work.tile([P, CHUNK_HEADS, PAIRS, 2, 2], F32)
+            if place == 0 or number == 0:
+                products = work.tile([P, 2, CHUNK_HEADS, PAIRS, 2, 2], F32)
+                filling["products"] = products
+            products = filling["products"]
             for h in range(CHUNK_HEADS):
                 nc.vector.scalar_tensor_tensor(
-                    out=products[:, h].rearrange("p j s e -> p (j s) e"),
+                    out=products[:, place, h].rearrange("p j s e -> p (j s) e"),
                     in0=acc[:, h * HEAD : (h + 1) * HEAD].unsqueeze(2).to_broadcast([P, HEAD, 2]),
                     scalar=r[:, h : h + 1],
                     in1=table[:, i].rearrange("p j s e -> p (j s) e"),
                     op0=ALU.mult,
                     op1=ALU.mult,
                 )
-            rotated = work.tile([P, CHUNK_HEADS, PAIRS, 2], F32)
+            if place == 0 and number < TOKEN_TILES * CHUNKS - 1:
+                return
+            first = place if number == 0 else 0
+            rotated = work.tile([P, 2, CHUNK_HEADS, PAIRS, 2], F32)
             nc.gpsimd.tensor_tensor(
-                out=rotated[:], in0=products[:, :, :, 0, :], in1=products[:, :, :, 1, :], op=ALU.add
+                out=rotated[:, first : place + 1],
+                in0=products[:, first : place + 1, :, :, 0, :],
+                in1=products[:, first : place + 1, :, :, 1, :],
+                op=ALU.add,
             )
             nc.sync.dma_start(
-                out=out_rows[:, i, c * CHUNK : (c + 1) * CHUNK],
-                in_=rotated[:].rearrange("p h j e -> p (h j e)"),
+                out=out_flat[:, (number - place + first) * CHUNK : (number + 1) * CHUNK],
+                in_=rotated[:, first : place + 1].rearrange("p n h j e -> p (n h j e)"),
             )
 
         transpose_and_quantise(0)

@@ -29,6 +29,8 @@ CHUNK = 512
 CHUNKS = FEATURES // CHUNK
 CHUNK_HEADS = CHUNK // HEAD
 SQUARE_SLOTS = 8
+SUM_GROUPS = [1] + [2] * 14 + [1, 1, 1]
+assert sum(SUM_GROUPS) == TOKEN_TILES * CHUNKS
 
 FLOPS = 2 * TOKENS * K * FEATURES
 
@@ -49,8 +51,7 @@ def tile_mla_pb_kernel(tc, x, wq_words, wq_scales, q_norm_w, freqs_cos, freqs_si
         stage = ctx.enter_context(tc.tile_pool(name="stage", bufs=2))
         small = ctx.enter_context(tc.tile_pool(name="small", bufs=8))
         work = ctx.enter_context(tc.tile_pool(name="work", bufs=4))
-        xt_pool = ctx.enter_context(tc.psum_pool(name="xt", bufs=2))
-        acc_pool = ctx.enter_context(tc.psum_pool(name="acc", bufs=6))
+        banks = ctx.enter_context(tc.psum_pool(name="banks", bufs=8))
 
         x_sb = keep.tile([P, TOKEN_TILES, K], BF16)
         x_codes = keep.tile([P, TOKEN_TILES, PASSES * P], U32, align_bytes=64)
@@ -101,7 +102,7 @@ def tile_mla_pb_kernel(tc, x, wq_words, wq_scales, q_norm_w, freqs_cos, freqs_si
             load_x(i)
 
         def spread_gain():
-            gain_ps = acc_pool.tile([P, CHUNK], F32, tag="acc")
+            gain_ps = banks.tile([P, CHUNK], F32, tag="bank")
             nc.tensor.matmul(out=gain_ps[:, 0:HEAD], lhsT=ones[:], rhs=gain_row[:], start=True, stop=True)
             gain_pairs = gain_ps[:, 0:HEAD].rearrange("p (j s) -> p j s", s=2)
             nc.vector.tensor_copy(out=factors[:, :, :, 1], in_=gain_pairs)
@@ -126,7 +127,7 @@ def tile_mla_pb_kernel(tc, x, wq_words, wq_scales, q_norm_w, freqs_cos, freqs_si
             grouped = stage.tile([P, 4 * PASSES * P], BF16, align_bytes=64)
             grouped_words = grouped[:].bitcast(F32).rearrange("p (g r u) -> p g r u", g=PASSES, u=2)
             for g0 in range(0, PASSES, 2):
-                xt = xt_pool.tile([P, 2, 2, P], F32)
+                xt = banks.tile([P, 2, 2, P], F32, tag="bank")
                 for g in range(g0, g0 + 2):
                     for u in range(2):
                         nc.tensor.transpose(
@@ -140,7 +141,7 @@ def tile_mla_pb_kernel(tc, x, wq_words, wq_scales, q_norm_w, freqs_cos, freqs_si
             )
 
         def project(i, c):
-            acc = acc_pool.tile([P, CHUNK], F32, tag="acc")
+            acc = banks.tile([P, CHUNK], F32, tag="bank")
             for g in range(PASSES):
                 nc.tensor.matmul_mx(
                     out=acc[:],
@@ -161,16 +162,21 @@ def tile_mla_pb_kernel(tc, x, wq_words, wq_scales, q_norm_w, freqs_cos, freqs_si
                 )
             return i, c, acc, sum_sq
 
+        group_of = {}
+        for size in SUM_GROUPS:
+            first = len(group_of)
+            for place in range(size):
+                group_of[first + place] = (place, size)
         filling = {}
 
         def rotate(i, c, acc, sum_sq):
             number = i * CHUNKS + c
-            place = (number + 1) % 2
+            place, size = group_of[number]
             r = small.tile([P, CHUNK_HEADS], F32)
             nc.scalar.activation(
                 out=r[:], in_=sum_sq[:], func=ACT.Abs_reciprocal_sqrt, scale=1.0 / HEAD, bias=eps[:]
             )
-            if place == 0 or number == 0:
+            if place == 0:
                 products = work.tile([P, 2, CHUNK_HEADS, PAIRS, 2, 2], F32)
                 filling["products"] = products
             products = filling["products"]
@@ -183,19 +189,18 @@ def tile_mla_pb_kernel(tc, x, wq_words, wq_scales, q_norm_w, freqs_cos, freqs_si
                     op0=ALU.mult,
                     op1=ALU.mult,
                 )
-            if place == 0 and number < TOKEN_TILES * CHUNKS - 1:
+            if place < size - 1:
                 return
-            first = place if number == 0 else 0
             rotated = work.tile([P, 2, CHUNK_HEADS, PAIRS, 2], F32)
             nc.gpsimd.tensor_tensor(
-                out=rotated[:, first : place + 1],
-                in0=products[:, first : place + 1, :, :, 0, :],
-                in1=products[:, first : place + 1, :, :, 1, :],
+                out=rotated[:, 0:size],
+                in0=products[:, 0:size, :, :, 0, :],
+                in1=products[:, 0:size, :, :, 1, :],
                 op=ALU.add,
             )
             nc.sync.dma_start(
-                out=out_flat[:, (number - place + first) * CHUNK : (number + 1) * CHUNK],
-                in_=rotated[:, first : place + 1].rearrange("p n h j e -> p (n h j e)"),
+                out=out_flat[:, (number - place) * CHUNK : (number + 1) * CHUNK],
+                in_=rotated[:, 0:size].rearrange("p n h j e -> p (n h j e)"),
             )
 
         transpose_and_quantise(0)

@@ -192,6 +192,19 @@ def tile_mla_pb_kernel(tc, x, wq_words, wq_scales, q_norm_w, freqs_cos, freqs_si
             if place < size - 1:
                 return
             rotated = work.tile([P, 2, CHUNK_HEADS, PAIRS, 2], F32)
+            if number == TOKEN_TILES * CHUNKS - 1:
+                for half in range(0, CHUNK_HEADS, 2):
+                    nc.vector.tensor_tensor(
+                        out=rotated[:, 0, half : half + 2],
+                        in0=products[:, 0, half : half + 2, :, 0, :],
+                        in1=products[:, 0, half : half + 2, :, 1, :],
+                        op=ALU.add,
+                    )
+                    nc.sync.dma_start(
+                        out=out_flat[:, number * CHUNK + half * HEAD : number * CHUNK + (half + 2) * HEAD],
+                        in_=rotated[:, 0, half : half + 2].rearrange("p h j e -> p (h j e)"),
+                    )
+                return
             nc.gpsimd.tensor_tensor(
                 out=rotated[:, 0:size],
                 in0=products[:, 0:size, :, :, 0, :],

@@ -122,7 +122,7 @@ def tile_mla_pb_kernel(tc, x, wq_words, wq_scales, q_norm_w, freqs_cos, freqs_si
                 op=ALU.mult,
             )
 
-        def transpose_and_quantise(i):
+        def transpose_and_quantise(i, calls):
             words = x_sb[:, i, :].bitcast(F32)
             grouped = stage.tile([P, 4 * PASSES * P], BF16, align_bytes=64)
             grouped_words = grouped[:].bitcast(F32).rearrange("p (g r u) -> p g r u", g=PASSES, u=2)
@@ -136,9 +136,16 @@ def tile_mla_pb_kernel(tc, x, wq_words, wq_scales, q_norm_w, freqs_cos, freqs_si
                 nc.scalar.copy(
                     out=grouped_words[:, g0 : g0 + 2, :, :], in_=xt[:].rearrange("p g u r -> p g r u")
                 )
-            nc.vector.quantize_mx(
-                out=x_codes[:, i, :].bitcast(FP8X4), scales=x_scales[:, i, :], in_=grouped[:]
-            )
+                if calls == 2:
+                    nc.vector.quantize_mx(
+                        out=x_codes[:, i, g0 * P : (g0 + 2) * P].bitcast(FP8X4),
+                        scales=x_scales[:, i, g0 * P : (g0 + 2) * P],
+                        in_=grouped[:, g0 * 4 * P : (g0 + 2) * 4 * P],
+                    )
+            if calls == 1:
+                nc.vector.quantize_mx(
+                    out=x_codes[:, i, :].bitcast(FP8X4), scales=x_scales[:, i, :], in_=grouped[:]
+                )
 
         def project(i, c):
             acc = banks.tile([P, CHUNK], F32, tag="bank")
@@ -192,19 +199,6 @@ def tile_mla_pb_kernel(tc, x, wq_words, wq_scales, q_norm_w, freqs_cos, freqs_si
             if place < size - 1:
                 return
             rotated = work.tile([P, 2, CHUNK_HEADS, PAIRS, 2], F32)
-            if number == TOKEN_TILES * CHUNKS - 1:
-                for half in range(0, CHUNK_HEADS, 2):
-                    nc.vector.tensor_tensor(
-                        out=rotated[:, 0, half : half + 2],
-                        in0=products[:, 0, half : half + 2, :, 0, :],
-                        in1=products[:, 0, half : half + 2, :, 1, :],
-                        op=ALU.add,
-                    )
-                    nc.sync.dma_start(
-                        out=out_flat[:, number * CHUNK + half * HEAD : number * CHUNK + (half + 2) * HEAD],
-                        in_=rotated[:, 0, half : half + 2].rearrange("p h j e -> p (h j e)"),
-                    )
-                return
             nc.gpsimd.tensor_tensor(
                 out=rotated[:, 0:size],
                 in0=products[:, 0:size, :, :, 0, :],
@@ -216,12 +210,62 @@ def tile_mla_pb_kernel(tc, x, wq_words, wq_scales, q_norm_w, freqs_cos, freqs_si
                 in_=rotated[:, 0:size].rearrange("p n h j e -> p (n h j e)"),
             )
 
-        transpose_and_quantise(0)
+        def last_chunk(i, c):
+            sum_sq = small.tile([P, CHUNK_HEADS], F32)
+            r = small.tile([P, CHUNK_HEADS], F32)
+            products = work.tile([P, 2, CHUNK_HEADS, PAIRS, 2, 2], F32)
+            rotated = work.tile([P, 2, CHUNK_HEADS, PAIRS, 2], F32)
+            for h in range(CHUNK_HEADS):
+                acc = banks.tile([P, CHUNK], F32, tag="bank")
+                for g in range(PASSES):
+                    nc.tensor.matmul_mx(
+                        out=acc[:, 0:HEAD],
+                        lhsT=x_codes[:, i, g * P : (g + 1) * P].bitcast(FP8X4),
+                        lhsT_scale=x_scales[:, i, g * P : (g + 1) * P],
+                        rhs=w_words[:, c, g, h * 2 * HEAD : (h + 1) * 2 * HEAD].bitcast(FP4X4),
+                        rhs_scale=w_scales[:, g, c * CHUNK + h * HEAD : c * CHUNK + (h + 1) * HEAD],
+                        start=(g == 0),
+                        stop=(g == PASSES - 1),
+                    )
+                nc.scalar.activation(
+                    out=squares[:, h, :], in_=acc[:, 0:HEAD], func=ACT.Square, accum_out=sum_sq[:, h : h + 1]
+                )
+                nc.scalar.activation(
+                    out=r[:, h : h + 1],
+                    in_=sum_sq[:, h : h + 1],
+                    func=ACT.Abs_reciprocal_sqrt,
+                    scale=1.0 / HEAD,
+                    bias=eps[:],
+                )
+                nc.vector.scalar_tensor_tensor(
+                    out=products[:, 0, h].rearrange("p j s e -> p (j s) e"),
+                    in0=acc[:, 0:HEAD].unsqueeze(2).to_broadcast([P, HEAD, 2]),
+                    scalar=r[:, h : h + 1],
+                    in1=table[:, i].rearrange("p j s e -> p (j s) e"),
+                    op0=ALU.mult,
+                    op1=ALU.mult,
+                )
+            first = (i * CHUNKS + c) * CHUNK
+            for half in range(0, CHUNK_HEADS, 2):
+                nc.vector.tensor_tensor(
+                    out=rotated[:, 0, half : half + 2],
+                    in0=products[:, 0, half : half + 2, :, 0, :],
+                    in1=products[:, 0, half : half + 2, :, 1, :],
+                    op=ALU.add,
+                )
+                nc.sync.dma_start(
+                    out=out_flat[:, first + half * HEAD : first + (half + 2) * HEAD],
+                    in_=rotated[:, 0, half : half + 2].rearrange("p h j e -> p (h j e)"),
+                )
+
+        transpose_and_quantise(0, 2)
         spread_gain()
         build_table()
         waiting = None
         for i in range(TOKEN_TILES):
             for c in range(CHUNKS):
+                if i == TOKEN_TILES - 1 and c == CHUNKS - 1:
+                    break
                 projected = project(i, c)
                 if waiting is not None:
                     rotate(*waiting)
@@ -230,7 +274,8 @@ def tile_mla_pb_kernel(tc, x, wq_words, wq_scales, q_norm_w, freqs_cos, freqs_si
                     rotate(*waiting)
                     waiting = None
                 if i == 0 and c == 1:
-                    transpose_and_quantise(1)
+                    transpose_and_quantise(1, 1)
                 if c == CHUNKS - 1 and i + 2 < TOKEN_TILES:
-                    transpose_and_quantise(i + 2)
+                    transpose_and_quantise(i + 2, 1)
         rotate(*waiting)
+        last_chunk(TOKEN_TILES - 1, CHUNKS - 1)

@@ -29,7 +29,7 @@ CHUNK = 512
 CHUNKS = FEATURES // CHUNK
 CHUNK_HEADS = CHUNK // HEAD
 SQUARE_SLOTS = 8
-SUM_GROUPS = [1] + [2] * 14 + [1, 1, 1]
+SUM_GROUPS = [1] * 2 + [2] * 13 + [1] * 4
 assert sum(SUM_GROUPS) == TOKEN_TILES * CHUNKS
 
 FLOPS = 2 * TOKENS * K * FEATURES
@@ -50,14 +50,16 @@ def tile_mla_pb_kernel(tc, x, wq_words, wq_scales, q_norm_w, freqs_cos, freqs_si
         keep = ctx.enter_context(tc.tile_pool(name="keep", bufs=1))
         stage = ctx.enter_context(tc.tile_pool(name="stage", bufs=2))
         small = ctx.enter_context(tc.tile_pool(name="small", bufs=8))
-        work = ctx.enter_context(tc.tile_pool(name="work", bufs=4))
+        work = ctx.enter_context(tc.tile_pool(name="work", bufs=6))
         banks = ctx.enter_context(tc.psum_pool(name="banks", bufs=8))
 
         x_sb = keep.tile([P, TOKEN_TILES, K], BF16)
         x_codes = keep.tile([P, TOKEN_TILES, PASSES * P], U32, align_bytes=64)
         x_scales = keep.tile([P, TOKEN_TILES, PASSES * P], U8, align_bytes=64)
         w_words = keep.tile([P, CHUNKS, PASSES, 2 * CHUNK], U8, align_bytes=64)
-        w_scales = keep.tile([P, PASSES, FEATURES], U8, align_bytes=64)
+        w_scales = []
+        for c in range(CHUNKS):
+            w_scales.append(keep.tile([P, PASSES, CHUNK], U8, align_bytes=64, name="w_scales_%d" % c))
         trig = keep.tile([P, 4, TOKEN_TILES * PAIRS], BF16)
         factors = keep.tile([P, PAIRS, 2, 2], F32)
         table = keep.tile([P, TOKEN_TILES, PAIRS, 2, 2], F32)
@@ -68,18 +70,26 @@ def tile_mla_pb_kernel(tc, x, wq_words, wq_scales, q_norm_w, freqs_cos, freqs_si
         warm = keep.tile([P, 1], F32)
         squares = keep.tile([P, SQUARE_SLOTS, HEAD], F32)
 
+        def scale_words(c):
+            return w_scales[c][:].bitcast(I32)
+
         nc.vector.memset(eps[:], EPS)
         nc.vector.memset(gain_row[:], 0.0)
-        nc.vector.memset(w_scales[:].bitcast(I32), 0)
+        nc.vector.memset(scale_words(0), 0)
         nc.vector.memset(ones[:], 1.0)
+        for c in range(1, CHUNKS):
+            nc.vector.memset(scale_words(c), 0)
         make_identity(nc, ident[:])
 
         def load_x(i):
             nc.sync.dma_start(out=x_sb[:, i, :], in_=x_rows[:, i, :])
 
-        def load_w_scales():
+        def load_w_scales(c):
             for r in range(4):
-                nc.sync.dma_start(out=w_scales[r:P:32, :, :].bitcast(I32), in_=w_scales_dram[r:16:4, :, :])
+                nc.sync.dma_start(
+                    out=scale_words(c)[r:P:32],
+                    in_=w_scales_dram[r:16:4, :, c * CHUNK // 4 : (c + 1) * CHUNK // 4],
+                )
 
         def load_w(c):
             nc.sync.dma_start(
@@ -88,16 +98,18 @@ def tile_mla_pb_kernel(tc, x, wq_words, wq_scales, q_norm_w, freqs_cos, freqs_si
             )
 
         load_x(0)
+        load_w_scales(0)
         load_w(0)
-        load_w_scales()
-        nc.scalar.dma_start(out=gain_row[0:1, :], in_=q_norm_w.unsqueeze(0))
-        nc.scalar.dma_start(out=trig[:, 0, :], in_=cos_rows)
+        nc.sync.dma_start(out=trig[:, 0, :], in_=cos_rows)
+        nc.sync.dma_start(out=trig[:, 1, :], in_=sin_rows)
+        nc.gpsimd.dma_start(out=gain_row[0:1, :], in_=q_norm_w.unsqueeze(0))
         nc.scalar.activation(out=warm[:], in_=eps[:], func=ACT.Abs_reciprocal_sqrt)
-        nc.scalar.dma_start(out=trig[:, 1, :], in_=sin_rows)
+        load_w_scales(1)
         load_w(1)
         load_x(1)
-        load_w(2)
-        load_w(3)
+        for c in range(2, CHUNKS):
+            load_w_scales(c)
+            load_w(c)
         for i in range(2, TOKEN_TILES):
             load_x(i)
 
@@ -109,20 +121,18 @@ def tile_mla_pb_kernel(tc, x, wq_words, wq_scales, q_norm_w, freqs_cos, freqs_si
             nc.vector.tensor_copy(out=factors[:, :, 0, 0], in_=gain_pairs[:, :, 0])
             nc.vector.tensor_scalar_mul(out=factors[:, :, 1, 0], in0=gain_pairs[:, :, 1], scalar1=-1.0)
 
-        def build_table():
-            nc.scalar.copy(out=trig[:, 2, :], in_=trig[:, 1, :])
-            nc.scalar.copy(out=trig[:, 3, :], in_=trig[:, 0, :])
+        def build_table(first, end):
             nc.vector.tensor_tensor(
-                out=table[:].rearrange("p i j s e -> p i j (s e)"),
-                in0=trig[:].rearrange("p f (i j) -> p i j f", i=TOKEN_TILES),
+                out=table[:, first:end].rearrange("p i j s e -> p i j (s e)"),
+                in0=trig[:, :, first * PAIRS : end * PAIRS].rearrange("p f (i j) -> p i j f", j=PAIRS),
                 in1=factors[:]
                 .rearrange("p j s e -> p j (s e)")
                 .unsqueeze(1)
-                .to_broadcast([P, TOKEN_TILES, PAIRS, 4]),
+                .to_broadcast([P, end - first, PAIRS, 4]),
                 op=ALU.mult,
             )
 
-        def transpose_and_quantise(i, calls):
+        def transpose_x(i, copied):
             words = x_sb[:, i, :].bitcast(F32)
             grouped = stage.tile([P, 4 * PASSES * P], BF16, align_bytes=64)
             grouped_words = grouped[:].bitcast(F32).rearrange("p (g r u) -> p g r u", g=PASSES, u=2)
@@ -133,21 +143,22 @@ def tile_mla_pb_kernel(tc, x, wq_words, wq_scales, q_norm_w, freqs_cos, freqs_si
                         nc.tensor.transpose(
                             xt[:, g - g0, u, :], words[:, g * WORDS + u : (g + 1) * WORDS : 2], ident[:]
                         )
-                nc.scalar.copy(
-                    out=grouped_words[:, g0 : g0 + 2, :, :], in_=xt[:].rearrange("p g u r -> p g r u")
-                )
-                if calls == 2:
-                    nc.vector.quantize_mx(
-                        out=x_codes[:, i, g0 * P : (g0 + 2) * P].bitcast(FP8X4),
-                        scales=x_scales[:, i, g0 * P : (g0 + 2) * P],
-                        in_=grouped[:, g0 * 4 * P : (g0 + 2) * 4 * P],
+                for g in range(g0, g0 + 2, copied):
+                    nc.scalar.copy(
+                        out=grouped_words[:, g : g + copied, :, :],
+                        in_=xt[:, g - g0 : g - g0 + copied].rearrange("p g u r -> p g r u"),
                     )
-            if calls == 1:
+            return grouped
+
+        def quantise_x(i, grouped, quantised):
+            for g in range(0, PASSES, quantised):
                 nc.vector.quantize_mx(
-                    out=x_codes[:, i, :].bitcast(FP8X4), scales=x_scales[:, i, :], in_=grouped[:]
+                    out=x_codes[:, i, g * P : (g + quantised) * P].bitcast(FP8X4),
+                    scales=x_scales[:, i, g * P : (g + quantised) * P],
+                    in_=grouped[:, g * 4 * P : (g + quantised) * 4 * P],
                 )
 
-        def project(i, c):
+        def project(i, c, before):
             acc = banks.tile([P, CHUNK], F32, tag="bank")
             for g in range(PASSES):
                 nc.tensor.matmul_mx(
@@ -155,11 +166,12 @@ def tile_mla_pb_kernel(tc, x, wq_words, wq_scales, q_norm_w, freqs_cos, freqs_si
                     lhsT=x_codes[:, i, g * P : (g + 1) * P].bitcast(FP8X4),
                     lhsT_scale=x_scales[:, i, g * P : (g + 1) * P],
                     rhs=w_words[:, c, g, :].bitcast(FP4X4),
-                    rhs_scale=w_scales[:, g, c * CHUNK : (c + 1) * CHUNK],
+                    rhs_scale=w_scales[c][:, g, :],
                     start=(g == 0),
                     stop=(g == PASSES - 1),
                 )
             sum_sq = small.tile([P, CHUNK_HEADS], F32)
+            r = small.tile([P, CHUNK_HEADS], F32)
             for h in range(CHUNK_HEADS):
                 nc.scalar.activation(
                     out=squares[:, (c * CHUNK_HEADS + h) % SQUARE_SLOTS, :],
@@ -167,7 +179,14 @@ def tile_mla_pb_kernel(tc, x, wq_words, wq_scales, q_norm_w, freqs_cos, freqs_si
                     func=ACT.Square,
                     accum_out=sum_sq[:, h : h + 1],
                 )
-            return i, c, acc, sum_sq
+                if h == 0 and before is not None:
+                    invert(*before[3:])
+            return i, c, acc, sum_sq, r
+
+        def invert(sum_sq, r):
+            nc.scalar.activation(
+                out=r[:], in_=sum_sq[:], func=ACT.Abs_reciprocal_sqrt, scale=1.0 / HEAD, bias=eps[:]
+            )
 
         group_of = {}
         for size in SUM_GROUPS:
@@ -176,13 +195,9 @@ def tile_mla_pb_kernel(tc, x, wq_words, wq_scales, q_norm_w, freqs_cos, freqs_si
                 group_of[first + place] = (place, size)
         filling = {}
 
-        def rotate(i, c, acc, sum_sq):
+        def rotate(i, c, acc, sum_sq, r):
             number = i * CHUNKS + c
             place, size = group_of[number]
-            r = small.tile([P, CHUNK_HEADS], F32)
-            nc.scalar.activation(
-                out=r[:], in_=sum_sq[:], func=ACT.Abs_reciprocal_sqrt, scale=1.0 / HEAD, bias=eps[:]
-            )
             if place == 0:
                 products = work.tile([P, 2, CHUNK_HEADS, PAIRS, 2, 2], F32)
                 filling["products"] = products
@@ -210,26 +225,10 @@ def tile_mla_pb_kernel(tc, x, wq_words, wq_scales, q_norm_w, freqs_cos, freqs_si
                 in_=rotated[:, 0:size].rearrange("p n h j e -> p (n h j e)"),
             )
 
-        def last_chunk(i, c):
-            sum_sq = small.tile([P, CHUNK_HEADS], F32)
-            r = small.tile([P, CHUNK_HEADS], F32)
-            products = work.tile([P, 2, CHUNK_HEADS, PAIRS, 2, 2], F32)
-            rotated = work.tile([P, 2, CHUNK_HEADS, PAIRS, 2], F32)
-            for h in range(CHUNK_HEADS):
-                acc = banks.tile([P, CHUNK], F32, tag="bank")
-                for g in range(PASSES):
-                    nc.tensor.matmul_mx(
-                        out=acc[:, 0:HEAD],
-                        lhsT=x_codes[:, i, g * P : (g + 1) * P].bitcast(FP8X4),
-                        lhsT_scale=x_scales[:, i, g * P : (g + 1) * P],
-                        rhs=w_words[:, c, g, h * 2 * HEAD : (h + 1) * 2 * HEAD].bitcast(FP4X4),
-                        rhs_scale=w_scales[:, g, c * CHUNK + h * HEAD : c * CHUNK + (h + 1) * HEAD],
-                        start=(g == 0),
-                        stop=(g == PASSES - 1),
-                    )
-                nc.scalar.activation(
-                    out=squares[:, h, :], in_=acc[:, 0:HEAD], func=ACT.Square, accum_out=sum_sq[:, h : h + 1]
-                )
+        def last_two_chunks(i, waiting):
+            unfinished = []
+
+            def finish(c, h, acc, sum_sq, r, products):
                 nc.scalar.activation(
                     out=r[:, h : h + 1],
                     in_=sum_sq[:, h : h + 1],
@@ -245,37 +244,84 @@ def tile_mla_pb_kernel(tc, x, wq_words, wq_scales, q_norm_w, freqs_cos, freqs_si
                     op0=ALU.mult,
                     op1=ALU.mult,
                 )
-            first = (i * CHUNKS + c) * CHUNK
-            for half in range(0, CHUNK_HEADS, 2):
-                nc.vector.tensor_tensor(
-                    out=rotated[:, 0, half : half + 2],
-                    in0=products[:, 0, half : half + 2, :, 0, :],
-                    in1=products[:, 0, half : half + 2, :, 1, :],
+
+            def sum_heads(engine, c, h0, h1, products, rotated):
+                first = (i * CHUNKS + c) * CHUNK
+                engine.tensor_tensor(
+                    out=rotated[:, 0, h0:h1],
+                    in0=products[:, 0, h0:h1, :, 0, :],
+                    in1=products[:, 0, h0:h1, :, 1, :],
                     op=ALU.add,
                 )
                 nc.sync.dma_start(
-                    out=out_flat[:, first + half * HEAD : first + (half + 2) * HEAD],
-                    in_=rotated[:, 0, half : half + 2].rearrange("p h j e -> p (h j e)"),
+                    out=out_flat[:, first + h0 * HEAD : first + h1 * HEAD],
+                    in_=rotated[:, 0, h0:h1].rearrange("p h j e -> p (h j e)"),
                 )
 
-        transpose_and_quantise(0, 2)
+            for c in (CHUNKS - 2, CHUNKS - 1):
+                sum_sq = small.tile([P, CHUNK_HEADS], F32)
+                r = small.tile([P, CHUNK_HEADS], F32)
+                products = work.tile([P, 2, CHUNK_HEADS, PAIRS, 2, 2], F32)
+                rotated = work.tile([P, 2, CHUNK_HEADS, PAIRS, 2], F32)
+                for h in range(CHUNK_HEADS):
+                    acc = banks.tile([P, CHUNK], F32, tag="bank")
+                    for g in range(PASSES):
+                        nc.tensor.matmul_mx(
+                            out=acc[:, 0:HEAD],
+                            lhsT=x_codes[:, i, g * P : (g + 1) * P].bitcast(FP8X4),
+                            lhsT_scale=x_scales[:, i, g * P : (g + 1) * P],
+                            rhs=w_words[:, c, g, h * 2 * HEAD : (h + 1) * 2 * HEAD].bitcast(FP4X4),
+                            rhs_scale=w_scales[c][:, g, h * HEAD : (h + 1) * HEAD],
+                            start=(g == 0),
+                            stop=(g == PASSES - 1),
+                        )
+                    nc.scalar.activation(
+                        out=squares[:, (c * CHUNK_HEADS + h) % SQUARE_SLOTS, :],
+                        in_=acc[:, 0:HEAD],
+                        func=ACT.Square,
+                        accum_out=sum_sq[:, h : h + 1],
+                    )
+                    if waiting is not None:
+                        invert(*waiting[3:])
+                        rotate(*waiting)
+                        waiting = None
+                    if unfinished:
+                        finish(*unfinished.pop())
+                    if c == CHUNKS - 1 and h == 0:
+                        sum_heads(nc.gpsimd, CHUNKS - 2, 0, CHUNK_HEADS, before[0], before[1])
+                    unfinished.append((c, h, acc, sum_sq, r, products))
+                before = (products, rotated)
+            finish(*unfinished.pop())
+            for half in range(0, CHUNK_HEADS, 2):
+                sum_heads(nc.vector, CHUNKS - 1, half, half + 2, products, rotated)
+
+        quantise_x(0, transpose_x(0, 1), 1)
+        nc.scalar.copy(out=trig[:, 2, :], in_=trig[:, 1, :])
+        nc.scalar.copy(out=trig[:, 3, :], in_=trig[:, 0, :])
         spread_gain()
-        build_table()
+        build_table(0, 1)
         waiting = None
+        transposed = None
         for i in range(TOKEN_TILES):
             for c in range(CHUNKS):
-                if i == TOKEN_TILES - 1 and c == CHUNKS - 1:
+                if i == TOKEN_TILES - 1 and c == CHUNKS - 2:
                     break
-                projected = project(i, c)
+                projected = project(i, c, waiting)
                 if waiting is not None:
                     rotate(*waiting)
                 waiting = projected
-                if i == 0 and c == 0:
+                if c == 0 and transposed is not None:
+                    quantise_x(i + 1, transposed, PASSES)
+                    transposed = None
+                if i == 0 and c < 2:
+                    invert(*waiting[3:])
                     rotate(*waiting)
                     waiting = None
                 if i == 0 and c == 1:
-                    transpose_and_quantise(1, 1)
+                    quantise_x(1, transpose_x(1, 2), PASSES)
+                    build_table(1, TOKEN_TILES // 2)
+                if i == 0 and c == CHUNKS - 1:
+                    build_table(TOKEN_TILES // 2, TOKEN_TILES)
                 if c == CHUNKS - 1 and i + 2 < TOKEN_TILES:
-                    transpose_and_quantise(i + 2, 1)
-        rotate(*waiting)
-        last_chunk(TOKEN_TILES - 1, CHUNKS - 1)
+                    transposed = transpose_x(i + 2, 2)
+        last_two_chunks(TOKEN_TILES - 1, waiting)

@@ -58,37 +58,43 @@ def tile_mla_pb_kernel(tc, x, wq_words, wq_scales, q_norm_w, freqs_cos, freqs_si
         x_scales = keep.tile([P, TOKEN_TILES, PASSES * P], U8, align_bytes=64)
         w_words = keep.tile([P, CHUNKS, PASSES, 2 * CHUNK], U8, align_bytes=64)
         w_scales = []
-        for c in range(CHUNKS):
-            w_scales.append(keep.tile([P, PASSES, CHUNK], U8, align_bytes=64, name="w_scales_%d" % c))
+        for half in range(2):
+            w_scales.append(keep.tile([P, PASSES, FEATURES // 2], U8, align_bytes=64, name="w_scales_%d" % half))
         trig = keep.tile([P, 4, TOKEN_TILES * PAIRS], BF16)
         factors = keep.tile([P, PAIRS, 2, 2], F32)
         table = keep.tile([P, TOKEN_TILES, PAIRS, 2, 2], F32)
         gain_row = keep.tile([P, HEAD], BF16)
         ones = keep.tile([P, P], BF16)
+        zeros = keep.tile([P, CHUNK], BF16)
         ident = keep.tile([P, P], F32)
         eps = keep.tile([P, 1], F32)
         warm = keep.tile([P, 1], F32)
         squares = keep.tile([P, SQUARE_SLOTS, HEAD], F32)
 
-        def scale_words(c):
-            return w_scales[c][:].bitcast(I32)
+        def scale_words(half):
+            return w_scales[half][:].bitcast(I32)
+
+        def scales_of(c, g):
+            first = c % (CHUNKS // 2) * CHUNK
+            return w_scales[c // (CHUNKS // 2)][:, g, first : first + CHUNK]
 
         nc.vector.memset(eps[:], EPS)
         nc.vector.memset(gain_row[:], 0.0)
-        nc.vector.memset(scale_words(0), 0)
-        nc.vector.memset(ones[:], 1.0)
-        for c in range(1, CHUNKS):
-            nc.vector.memset(scale_words(c), 0)
+        nc.gpsimd.memset(zeros[:], 0.0)
+        nc.gpsimd.dma_start(out=gain_row[0:1, :], in_=q_norm_w.unsqueeze(0))
         make_identity(nc, ident[:])
+        nc.vector.memset(ones[:], 1.0)
+        for half in range(2):
+            nc.vector.memset(scale_words(half), 0)
 
         def load_x(i):
             nc.sync.dma_start(out=x_sb[:, i, :], in_=x_rows[:, i, :])
 
-        def load_w_scales(c):
+        def load_w_scales(half):
             for r in range(4):
                 nc.sync.dma_start(
-                    out=scale_words(c)[r:P:32],
-                    in_=w_scales_dram[r:16:4, :, c * CHUNK // 4 : (c + 1) * CHUNK // 4],
+                    out=scale_words(half)[r:P:32],
+                    in_=w_scales_dram[r:16:4, :, half * FEATURES // 8 : (half + 1) * FEATURES // 8],
                 )
 
         def load_w(c):
@@ -98,20 +104,23 @@ def tile_mla_pb_kernel(tc, x, wq_words, wq_scales, q_norm_w, freqs_cos, freqs_si
             )
 
         load_x(0)
-        load_w_scales(0)
         load_w(0)
+        load_w_scales(0)
+        load_w(1)
         nc.sync.dma_start(out=trig[:, 0, :], in_=cos_rows)
         nc.sync.dma_start(out=trig[:, 1, :], in_=sin_rows)
-        nc.gpsimd.dma_start(out=gain_row[0:1, :], in_=q_norm_w.unsqueeze(0))
         nc.scalar.activation(out=warm[:], in_=eps[:], func=ACT.Abs_reciprocal_sqrt)
-        load_w_scales(1)
-        load_w(1)
         load_x(1)
-        for c in range(2, CHUNKS):
-            load_w_scales(c)
-            load_w(c)
+        load_w_scales(1)
+        load_w(2)
+        load_w(3)
         for i in range(2, TOKEN_TILES):
             load_x(i)
+
+        def warm_up(count):
+            for n in range(count):
+                unread = banks.tile([P, CHUNK], F32, tag="bank")
+                nc.tensor.matmul(out=unread[:], lhsT=ones[:], rhs=zeros[:], start=True, stop=True)
 
         def spread_gain():
             gain_ps = banks.tile([P, CHUNK], F32, tag="bank")
@@ -121,8 +130,8 @@ def tile_mla_pb_kernel(tc, x, wq_words, wq_scales, q_norm_w, freqs_cos, freqs_si
             nc.vector.tensor_copy(out=factors[:, :, 0, 0], in_=gain_pairs[:, :, 0])
             nc.vector.tensor_scalar_mul(out=factors[:, :, 1, 0], in0=gain_pairs[:, :, 1], scalar1=-1.0)
 
-        def build_table(first, end):
-            nc.vector.tensor_tensor(
+        def build_table(engine, first, end):
+            engine.tensor_tensor(
                 out=table[:, first:end].rearrange("p i j s e -> p i j (s e)"),
                 in0=trig[:, :, first * PAIRS : end * PAIRS].rearrange("p f (i j) -> p i j f", j=PAIRS),
                 in1=factors[:]
@@ -166,7 +175,7 @@ def tile_mla_pb_kernel(tc, x, wq_words, wq_scales, q_norm_w, freqs_cos, freqs_si
                     lhsT=x_codes[:, i, g * P : (g + 1) * P].bitcast(FP8X4),
                     lhsT_scale=x_scales[:, i, g * P : (g + 1) * P],
                     rhs=w_words[:, c, g, :].bitcast(FP4X4),
-                    rhs_scale=w_scales[c][:, g, :],
+                    rhs_scale=scales_of(c, g),
                     start=(g == 0),
                     stop=(g == PASSES - 1),
                 )
@@ -271,7 +280,7 @@ def tile_mla_pb_kernel(tc, x, wq_words, wq_scales, q_norm_w, freqs_cos, freqs_si
                             lhsT=x_codes[:, i, g * P : (g + 1) * P].bitcast(FP8X4),
                             lhsT_scale=x_scales[:, i, g * P : (g + 1) * P],
                             rhs=w_words[:, c, g, h * 2 * HEAD : (h + 1) * 2 * HEAD].bitcast(FP4X4),
-                            rhs_scale=w_scales[c][:, g, h * HEAD : (h + 1) * HEAD],
+                            rhs_scale=scales_of(c, g)[:, h * HEAD : (h + 1) * HEAD],
                             start=(g == 0),
                             stop=(g == PASSES - 1),
                         )
@@ -295,33 +304,38 @@ def tile_mla_pb_kernel(tc, x, wq_words, wq_scales, q_norm_w, freqs_cos, freqs_si
             for half in range(0, CHUNK_HEADS, 2):
                 sum_heads(nc.vector, CHUNKS - 1, half, half + 2, products, rotated)
 
+        warm_up(4)
         quantise_x(0, transpose_x(0, 1), 1)
-        nc.scalar.copy(out=trig[:, 2, :], in_=trig[:, 1, :])
-        nc.scalar.copy(out=trig[:, 3, :], in_=trig[:, 0, :])
+        warm_up(2)
         spread_gain()
-        build_table(0, 1)
+        nc.vector.tensor_copy(out=trig[:, 3, :], in_=trig[:, 0, :])
+        nc.vector.tensor_copy(out=trig[:, 2, :], in_=trig[:, 1, :])
+        build_table(nc.vector, 0, 1)
+        build_table(nc.gpsimd, 1, TOKEN_TILES // 2)
         waiting = None
+        inverted = False
         transposed = None
         for i in range(TOKEN_TILES):
             for c in range(CHUNKS):
                 if i == TOKEN_TILES - 1 and c == CHUNKS - 2:
                     break
-                projected = project(i, c, waiting)
+                projected = project(i, c, None if inverted else waiting)
                 if waiting is not None:
                     rotate(*waiting)
                 waiting = projected
+                inverted = False
                 if c == 0 and transposed is not None:
                     quantise_x(i + 1, transposed, PASSES)
                     transposed = None
-                if i == 0 and c < 2:
+                if i == 0 and c < CHUNKS - 1:
                     invert(*waiting[3:])
                     rotate(*waiting)
                     waiting = None
                 if i == 0 and c == 1:
                     quantise_x(1, transpose_x(1, 2), PASSES)
-                    build_table(1, TOKEN_TILES // 2)
-                if i == 0 and c == CHUNKS - 1:
-                    build_table(TOKEN_TILES // 2, TOKEN_TILES)
+                    build_table(nc.gpsimd, TOKEN_TILES // 2, TOKEN_TILES)
                 if c == CHUNKS - 1 and i + 2 < TOKEN_TILES:
+                    invert(*waiting[3:])
+                    inverted = True
                     transposed = transpose_x(i + 2, 2)
         last_two_chunks(TOKEN_TILES - 1, waiting)

@@ -141,7 +141,7 @@ def tile_mla_pb_kernel(tc, x, wq_words, wq_scales, q_norm_w, freqs_cos, freqs_si
                 op=ALU.mult,
             )
 
-        def transpose_x(i, copied):
+        def transpose_x(i, copied, before=None):
             words = x_sb[:, i, :].bitcast(F32)
             grouped = stage.tile([P, 4 * PASSES * P], BF16, align_bytes=64)
             grouped_words = grouped[:].bitcast(F32).rearrange("p (g r u) -> p g r u", g=PASSES, u=2)
@@ -157,6 +157,8 @@ def tile_mla_pb_kernel(tc, x, wq_words, wq_scales, q_norm_w, freqs_cos, freqs_si
                         out=grouped_words[:, g : g + copied, :, :],
                         in_=xt[:, g - g0 : g - g0 + copied].rearrange("p g u r -> p g r u"),
                     )
+                if g0 == 0 and before is not None:
+                    invert(*before[3:])
             return grouped
 
         def quantise_x(i, grouped, quantised):
@@ -327,7 +329,7 @@ def tile_mla_pb_kernel(tc, x, wq_words, wq_scales, q_norm_w, freqs_cos, freqs_si
                 if c == 0 and transposed is not None:
                     quantise_x(i + 1, transposed, PASSES)
                     transposed = None
-                if i == 0 and c < CHUNKS - 1:
+                if i == 0 and c < 2:
                     invert(*waiting[3:])
                     rotate(*waiting)
                     waiting = None
@@ -335,7 +337,6 @@ def tile_mla_pb_kernel(tc, x, wq_words, wq_scales, q_norm_w, freqs_cos, freqs_si
                     quantise_x(1, transpose_x(1, 2), PASSES)
                     build_table(nc.gpsimd, TOKEN_TILES // 2, TOKEN_TILES)
                 if c == CHUNKS - 1 and i + 2 < TOKEN_TILES:
-                    invert(*waiting[3:])
+                    transposed = transpose_x(i + 2, 2, waiting)
                     inverted = True
-                    transposed = transpose_x(i + 2, 2)
         last_two_chunks(TOKEN_TILES - 1, waiting)

@@ -335,7 +335,7 @@ def tile_mla_pb_kernel(tc, x, wq_words, wq_scales, q_norm_w, freqs_cos, freqs_si
                     waiting = None
                 if i == 0 and c == 1:
                     quantise_x(1, transpose_x(1, 2), PASSES)
-                    build_table(nc.gpsimd, TOKEN_TILES // 2, TOKEN_TILES)
+                    build_table(nc.vector, TOKEN_TILES // 2, TOKEN_TILES)
                 if c == CHUNKS - 1 and i + 2 < TOKEN_TILES:
                     transposed = transpose_x(i + 2, 2, waiting)
                     inverted = True

@@ -29,7 +29,7 @@ CHUNK = 512
 CHUNKS = FEATURES // CHUNK
 CHUNK_HEADS = CHUNK // HEAD
 SQUARE_SLOTS = 8
-SUM_GROUPS = [1] * 2 + [2] * 13 + [1] * 4
+SUM_GROUPS = [1] * 2 + [2] * 14 + [1] * 2
 assert sum(SUM_GROUPS) == TOKEN_TILES * CHUNKS
 
 FLOPS = 2 * TOKENS * K * FEATURES
@@ -106,11 +106,11 @@ def tile_mla_pb_kernel(tc, x, wq_words, wq_scales, q_norm_w, freqs_cos, freqs_si
         load_x(0)
         load_w(0)
         load_w_scales(0)
-        load_w(1)
         nc.sync.dma_start(out=trig[:, 0, :], in_=cos_rows)
         nc.sync.dma_start(out=trig[:, 1, :], in_=sin_rows)
         nc.scalar.activation(out=warm[:], in_=eps[:], func=ACT.Abs_reciprocal_sqrt)
         load_x(1)
+        load_w(1)
         load_w_scales(1)
         load_w(2)
         load_w(3)
@@ -333,8 +333,9 @@ def tile_mla_pb_kernel(tc, x, wq_words, wq_scales, q_norm_w, freqs_cos, freqs_si
                     invert(*waiting[3:])
                     rotate(*waiting)
                     waiting = None
-                if i == 0 and c == 1:
+                if i == 0 and c == 0:
                     quantise_x(1, transpose_x(1, 2), PASSES)
+                if i == 0 and c == 1:
                     build_table(nc.vector, TOKEN_TILES // 2, TOKEN_TILES)
                 if c == CHUNKS - 1 and i + 2 < TOKEN_TILES:
                     transposed = transpose_x(i + 2, 2, waiting)

from contextlib import ExitStack

import concourse.mybir as mybir
from concourse.masks import make_identity

F32 = mybir.dt.float32
BF16 = mybir.dt.bfloat16
I32 = mybir.dt.int32
U32 = mybir.dt.uint32
U8 = mybir.dt.uint8
FP8X4 = mybir.dt.float8_e4m3fn_x4
FP4X4 = mybir.dt.float4_e2m1fn_x4
ACT = mybir.ActivationFunctionType
ALU = mybir.AluOpType

P = 128
TOKENS = 1024
K = 2048
FEATURES = 2048
HEAD = 128
PAIRS = HEAD // 2
EPS = 1e-6

TOKEN_TILES = TOKENS // P
K_PASS = 4 * P
PASSES = K // K_PASS
WORDS = K_PASS // 2
CHUNK = 512
CHUNKS = FEATURES // CHUNK
CHUNK_HEADS = CHUNK // HEAD
SQUARE_SLOTS = 8
SUM_GROUPS = [1] * 2 + [2] * 14 + [1] * 2
assert sum(SUM_GROUPS) == TOKEN_TILES * CHUNKS

FLOPS = 2 * TOKENS * K * FEATURES


def tile_mla_pb_kernel(tc, x, wq_words, wq_scales, q_norm_w, freqs_cos, freqs_sin, out):
    nc = tc.nc

    x_rows = x[0].rearrange("(p i) k -> p i k", i=TOKEN_TILES)
    out_flat = out[0].rearrange("(p i) h d -> p (i h d)", i=TOKEN_TILES)
    cos_rows = freqs_cos.rearrange("(p i) j -> p (i j)", i=TOKEN_TILES)
    sin_rows = freqs_sin.rearrange("(p i) j -> p (i j)", i=TOKEN_TILES)
    w_words_dram = wq_words.bitcast(I32).rearrange("g p n -> p g n")
    w_scales_dram = wq_scales.bitcast(I32).rearrange("g q n -> q g n")

    with ExitStack() as ctx:
        ctx.enter_context(tc.manual_schedule())
        keep = ctx.enter_context(tc.tile_pool(name="keep", bufs=1))
        stage = ctx.enter_context(tc.tile_pool(name="stage", bufs=2))
        small = ctx.enter_context(tc.tile_pool(name="small", bufs=8))
        work = ctx.enter_context(tc.tile_pool(name="work", bufs=6))
        banks = ctx.enter_context(tc.psum_pool(name="banks", bufs=8))

        x_sb = keep.tile([P, TOKEN_TILES, K], BF16)
        x_codes = keep.tile([P, TOKEN_TILES, PASSES * P], U32, align_bytes=64)
        x_scales = keep.tile([P, TOKEN_TILES, PASSES * P], U8, align_bytes=64)
        w_words = keep.tile([P, CHUNKS, PASSES, 2 * CHUNK], U8, align_bytes=64)
        w_scales = []
        for half in range(2):
            w_scales.append(keep.tile([P, PASSES, FEATURES // 2], U8, align_bytes=64, name="w_scales_%d" % half))
        trig = keep.tile([P, 4, TOKEN_TILES * PAIRS], BF16)
        factors = keep.tile([P, PAIRS, 2, 2], F32)
        table = keep.tile([P, TOKEN_TILES, PAIRS, 2, 2], F32)
        gain_row = keep.tile([P, HEAD], BF16)
        ones = keep.tile([P, P], BF16)
        zeros = keep.tile([P, CHUNK], BF16)
        ident = keep.tile([P, P], F32)
        eps = keep.tile([P, 1], F32)
        warm = keep.tile([P, 1], F32)
        squares = keep.tile([P, SQUARE_SLOTS, HEAD], F32)

        def scale_words(half):
            return w_scales[half][:].bitcast(I32)

        def scales_of(c, g):
            first = c % (CHUNKS // 2) * CHUNK
            return w_scales[c // (CHUNKS // 2)][:, g, first : first + CHUNK]

        nc.vector.memset(eps[:], EPS)
        nc.vector.memset(gain_row[:], 0.0)
        nc.gpsimd.memset(zeros[:], 0.0)
        nc.gpsimd.dma_start(out=gain_row[0:1, :], in_=q_norm_w.unsqueeze(0))
        make_identity(nc, ident[:])
        nc.vector.memset(ones[:], 1.0)
        for half in range(2):
            nc.vector.memset(scale_words(half), 0)

        def load_x(i):
            nc.sync.dma_start(out=x_sb[:, i, :], in_=x_rows[:, i, :])

        def load_w_scales(half):
            for r in range(4):
                nc.sync.dma_start(
                    out=scale_words(half)[r:P:32],
                    in_=w_scales_dram[r:16:4, :, half * FEATURES // 8 : (half + 1) * FEATURES // 8],
                )

        def load_w(c):
            nc.sync.dma_start(
                out=w_words[:, c, :, :].bitcast(I32),
                in_=w_words_dram[:, :, c * CHUNK // 2 : (c + 1) * CHUNK // 2],
            )

        load_x(0)
        load_w(0)
        load_w_scales(0)
        nc.sync.dma_start(out=trig[:, 0, :], in_=cos_rows)
        nc.sync.dma_start(out=trig[:, 1, :], in_=sin_rows)
        nc.scalar.activation(out=warm[:], in_=eps[:], func=ACT.Abs_reciprocal_sqrt)
        load_x(1)
        load_w(1)
        load_w_scales(1)
        load_w(2)
        load_w(3)
        for i in range(2, TOKEN_TILES):
            load_x(i)

        def warm_up(count):
            for n in range(count):
                unread = banks.tile([P, CHUNK], F32, tag="bank")
                nc.tensor.matmul(out=unread[:], lhsT=ones[:], rhs=zeros[:], start=True, stop=True)

        def spread_gain():
            gain_ps = banks.tile([P, CHUNK], F32, tag="bank")
            nc.tensor.matmul(out=gain_ps[:, 0:HEAD], lhsT=ones[:], rhs=gain_row[:], start=True, stop=True)
            gain_pairs = gain_ps[:, 0:HEAD].rearrange("p (j s) -> p j s", s=2)
            nc.vector.tensor_copy(out=factors[:, :, :, 1], in_=gain_pairs)
            nc.vector.tensor_copy(out=factors[:, :, 0, 0], in_=gain_pairs[:, :, 0])
            nc.vector.tensor_scalar_mul(out=factors[:, :, 1, 0], in0=gain_pairs[:, :, 1], scalar1=-1.0)

        def build_table(engine, first, end):
            engine.tensor_tensor(
                out=table[:, first:end].rearrange("p i j s e -> p i j (s e)"),
                in0=trig[:, :, first * PAIRS : end * PAIRS].rearrange("p f (i j) -> p i j f", j=PAIRS),
                in1=factors[:]
                .rearrange("p j s e -> p j (s e)")
                .unsqueeze(1)
                .to_broadcast([P, end - first, PAIRS, 4]),
                op=ALU.mult,
            )

        def transpose_x(i, copied, before=None):
            words = x_sb[:, i, :].bitcast(F32)
            grouped = stage.tile([P, 4 * PASSES * P], BF16, align_bytes=64)
            grouped_words = grouped[:].bitcast(F32).rearrange("p (g r u) -> p g r u", g=PASSES, u=2)
            for g0 in range(0, PASSES, 2):
                xt = banks.tile([P, 2, 2, P], F32, tag="bank")
                for g in range(g0, g0 + 2):
                    for u in range(2):
                        nc.tensor.transpose(
                            xt[:, g - g0, u, :], words[:, g * WORDS + u : (g + 1) * WORDS : 2], ident[:]
                        )
                for g in range(g0, g0 + 2, copied):
                    nc.scalar.copy(
                        out=grouped_words[:, g : g + copied, :, :],
                        in_=xt[:, g - g0 : g - g0 + copied].rearrange("p g u r -> p g r u"),
                    )
                if g0 == 0 and before is not None:
                    invert(*before[3:])
            return grouped

        def quantise_x(i, grouped, quantised):
            for g in range(0, PASSES, quantised):
                nc.vector.quantize_mx(
                    out=x_codes[:, i, g * P : (g + quantised) * P].bitcast(FP8X4),
                    scales=x_scales[:, i, g * P : (g + quantised) * P],
                    in_=grouped[:, g * 4 * P : (g + quantised) * 4 * P],
                )

        def project(i, c, before):
            acc = banks.tile([P, CHUNK], F32, tag="bank")
            for g in range(PASSES):
                nc.tensor.matmul_mx(
                    out=acc[:],
                    lhsT=x_codes[:, i, g * P : (g + 1) * P].bitcast(FP8X4),
                    lhsT_scale=x_scales[:, i, g * P : (g + 1) * P],
                    rhs=w_words[:, c, g, :].bitcast(FP4X4),
                    rhs_scale=scales_of(c, g),
                    start=(g == 0),
                    stop=(g == PASSES - 1),
                )
            sum_sq = small.tile([P, CHUNK_HEADS], F32)
            r = small.tile([P, CHUNK_HEADS], F32)
            for h in range(CHUNK_HEADS):
                nc.scalar.activation(
                    out=squares[:, (c * CHUNK_HEADS + h) % SQUARE_SLOTS, :],
                    in_=acc[:, h * HEAD : (h + 1) * HEAD],
                    func=ACT.Square,
                    accum_out=sum_sq[:, h : h + 1],
                )
                if h == 0 and before is not None:
                    invert(*before[3:])
            return i, c, acc, sum_sq, r

        def invert(sum_sq, r):
            nc.scalar.activation(
                out=r[:], in_=sum_sq[:], func=ACT.Abs_reciprocal_sqrt, scale=1.0 / HEAD, bias=eps[:]
            )

        group_of = {}
        for size in SUM_GROUPS:
            first = len(group_of)
            for place in range(size):
                group_of[first + place] = (place, size)
        filling = {}

        def rotate(i, c, acc, sum_sq, r):
            number = i * CHUNKS + c
            place, size = group_of[number]
            if place == 0:
                products = work.tile([P, 2, CHUNK_HEADS, PAIRS, 2, 2], F32)
                filling["products"] = products
            products = filling["products"]
            for h in range(CHUNK_HEADS):
                nc.vector.scalar_tensor_tensor(
                    out=products[:, place, h].rearrange("p j s e -> p (j s) e"),
                    in0=acc[:, h * HEAD : (h + 1) * HEAD].unsqueeze(2).to_broadcast([P, HEAD, 2]),
                    scalar=r[:, h : h + 1],
                    in1=table[:, i].rearrange("p j s e -> p (j s) e"),
                    op0=ALU.mult,
                    op1=ALU.mult,
                )
            if place < size - 1:
                return
            rotated = work.tile([P, 2, CHUNK_HEADS, PAIRS, 2], F32)
            nc.gpsimd.tensor_tensor(
                out=rotated[:, 0:size],
                in0=products[:, 0:size, :, :, 0, :],
                in1=products[:, 0:size, :, :, 1, :],
                op=ALU.add,
            )
            nc.sync.dma_start(
                out=out_flat[:, (number - place) * CHUNK : (number + 1) * CHUNK],
                in_=rotated[:, 0:size].rearrange("p n h j e -> p (n h j e)"),
            )

        def last_two_chunks(i, waiting):
            unfinished = []

            def finish(c, h, acc, sum_sq, r, products):
                nc.scalar.activation(
                    out=r[:, h : h + 1],
                    in_=sum_sq[:, h : h + 1],
                    func=ACT.Abs_reciprocal_sqrt,
                    scale=1.0 / HEAD,
                    bias=eps[:],
                )
                nc.vector.scalar_tensor_tensor(
                    out=products[:, 0, h].rearrange("p j s e -> p (j s) e"),
                    in0=acc[:, 0:HEAD].unsqueeze(2).to_broadcast([P, HEAD, 2]),
                    scalar=r[:, h : h + 1],
                    in1=table[:, i].rearrange("p j s e -> p (j s) e"),
                    op0=ALU.mult,
                    op1=ALU.mult,
                )

            def sum_heads(engine, c, h0, h1, products, rotated):
                first = (i * CHUNKS + c) * CHUNK
                engine.tensor_tensor(
                    out=rotated[:, 0, h0:h1],
                    in0=products[:, 0, h0:h1, :, 0, :],
                    in1=products[:, 0, h0:h1, :, 1, :],
                    op=ALU.add,
                )
                nc.sync.dma_start(
                    out=out_flat[:, first + h0 * HEAD : first + h1 * HEAD],
                    in_=rotated[:, 0, h0:h1].rearrange("p h j e -> p (h j e)"),
                )

            for c in (CHUNKS - 2, CHUNKS - 1):
                sum_sq = small.tile([P, CHUNK_HEADS], F32)
                r = small.tile([P, CHUNK_HEADS], F32)
                products = work.tile([P, 2, CHUNK_HEADS, PAIRS, 2, 2], F32)
                rotated = work.tile([P, 2, CHUNK_HEADS, PAIRS, 2], F32)
                for h in range(CHUNK_HEADS):
                    acc = banks.tile([P, CHUNK], F32, tag="bank")
                    for g in range(PASSES):
                        nc.tensor.matmul_mx(
                            out=acc[:, 0:HEAD],
                            lhsT=x_codes[:, i, g * P : (g + 1) * P].bitcast(FP8X4),
                            lhsT_scale=x_scales[:, i, g * P : (g + 1) * P],
                            rhs=w_words[:, c, g, h * 2 * HEAD : (h + 1) * 2 * HEAD].bitcast(FP4X4),
                            rhs_scale=scales_of(c, g)[:, h * HEAD : (h + 1) * HEAD],
                            start=(g == 0),
                            stop=(g == PASSES - 1),
                        )
                    nc.scalar.activation(
                        out=squares[:, (c * CHUNK_HEADS + h) % SQUARE_SLOTS, :],
                        in_=acc[:, 0:HEAD],
                        func=ACT.Square,
                        accum_out=sum_sq[:, h : h + 1],
                    )
                    if waiting is not None:
                        invert(*waiting[3:])
                        rotate(*waiting)
                        waiting = None
                    if unfinished:
                        finish(*unfinished.pop())
                    if c == CHUNKS - 1 and h == 0:
                        sum_heads(nc.gpsimd, CHUNKS - 2, 0, CHUNK_HEADS, before[0], before[1])
                    unfinished.append((c, h, acc, sum_sq, r, products))
                before = (products, rotated)
            finish(*unfinished.pop())
            for half in range(0, CHUNK_HEADS, 2):
                sum_heads(nc.vector, CHUNKS - 1, half, half + 2, products, rotated)

        warm_up(4)
        quantise_x(0, transpose_x(0, 1), 1)
        warm_up(2)
        spread_gain()
        nc.vector.tensor_copy(out=trig[:, 3, :], in_=trig[:, 0, :])
        nc.vector.tensor_copy(out=trig[:, 2, :], in_=trig[:, 1, :])
        build_table(nc.vector, 0, 1)
        build_table(nc.gpsimd, 1, TOKEN_TILES // 2)
        waiting = None
        inverted = False
        transposed = None
        for i in range(TOKEN_TILES):
            for c in range(CHUNKS):
                if i == TOKEN_TILES - 1 and c == CHUNKS - 2:
                    break
                projected = project(i, c, None if inverted else waiting)
                if waiting is not None:
                    rotate(*waiting)
                waiting = projected
                inverted = False
                if c == 0 and transposed is not None:
                    quantise_x(i + 1, transposed, PASSES)
                    transposed = None
                if i == 0 and c < 2:
                    invert(*waiting[3:])
                    rotate(*waiting)
                    waiting = None
                if i == 0 and c == 0:
                    quantise_x(1, transpose_x(1, 2), PASSES)
                if i == 0 and c == 1:
                    build_table(nc.vector, TOKEN_TILES // 2, TOKEN_TILES)
                if c == CHUNKS - 1 and i + 2 < TOKEN_TILES:
                    transposed = transpose_x(i + 2, 2, waiting)
                    inverted = True
        last_two_chunks(TOKEN_TILES - 1, waiting)
